import numpy as np
import ml_dtypes


def mxq(x, axis, fmt="e4m3"):
    dtype, down = {"e4m3": (ml_dtypes.float8_e4m3fn, 7), "e5m2": (ml_dtypes.float8_e5m2, 14)}[fmt]
    v = np.moveaxis(np.asarray(x, np.float32).astype(ml_dtypes.bfloat16).astype(np.float64), axis, -1)
    blocks = v.reshape(v.shape[:-1] + (-1, 32))
    amax = np.abs(blocks).max(-1, keepdims=True)
    byte = np.maximum(np.where(amax > 0, np.frexp(amax)[1] - 1 + 127, 0) - down, 1)
    scale = np.exp2(byte - 127.0)
    codes = (blocks / scale).astype(np.float32).astype(dtype).astype(np.float64)
    return np.moveaxis((codes * scale).reshape(v.shape), -1, axis)


WIDE = False


def mx_kscale(k):
    if not WIDE:
        return np.ones(k)
    levels = np.array([10, -10, 5, -5, 0])
    if k % 512:
        return np.exp2(np.random.permutation(np.resize(levels, k // 32))).repeat(32)
    a = np.empty((k // 512, 16))
    for p in range(k // 512):
        a[p, :8] = np.random.permutation(np.resize(levels, 8))
        for g in range(8):
            far = levels[np.abs(levels - a[p, g]) >= 10]
            a[p, g + 8] = far[np.random.randint(len(far))]
    return np.exp2(a.ravel()).repeat(32)


BF16 = ml_dtypes.bfloat16


def bf(x):
    return np.asarray(x, np.float32).astype(BF16)


def f64(x):
    return np.asarray(x).astype(np.float64)


B, S, DV, D, H, A = 2, 256, 1024, 1024, 8, 64
LN_EPS = 1e-3


def setup_inputs():
    s = mx_kscale(DV)
    return {
        "attn": bf(np.random.standard_normal((B, H, S, DV)) * 0.4 * s),
        "Wo": bf(np.random.standard_normal((H, DV, D)) * 0.6 / np.sqrt(DV * H) / s[None, :, None]),
        "bo": bf(np.random.standard_normal((H, D)) * 0.12 / np.sqrt(H)),
        "query_inputs": bf(np.random.standard_normal((B, S, D)) * 0.1),
        "gamma": bf(1.0 + 0.1 * np.random.standard_normal(D)),
        "beta": bf(0.1 * np.random.standard_normal(D)),
    }


def core(attn, Wo, bo, query_inputs, gamma, beta):
    pre = mxq(f64(attn), 3, "e4m3") @ mxq(f64(Wo), 1, "e4m3")
    head_out = np.maximum(pre + f64(bo)[None, :, None, :], 0.0)
    x = f64(query_inputs) + head_out.sum(axis=1)
    mean = x.mean(axis=-1, keepdims=True)
    var = x.var(axis=-1, keepdims=True)
    return f64(gamma) * (x - mean) / np.sqrt(var + LN_EPS) + f64(beta)


def e4m3fn_bytes(y):
    return np.clip(np.asarray(y, np.float64), -448.0, 448.0).astype(np.float32).astype(ml_dtypes.float8_e4m3fn).view(np.uint8)


Y_SCALE = 220.0


def reference(attn, Wo, bo, query_inputs, gamma, beta):
    out = core(attn, Wo, bo, query_inputs, gamma, beta)
    return out, e4m3fn_bytes(out * Y_SCALE)

@@ -1,0 +1,338 @@
+from contextlib import ExitStack
+
+import concourse.mybir as mybir
+from concourse.masks import make_identity
+
+B, H, S, K, D = 2, 8, 256, 1024, 1024
+FLOPS = 2 * B * H * S * K * D
+
+F32 = mybir.dt.float32
+BF16 = mybir.dt.bfloat16
+U32 = mybir.dt.uint32
+U8 = mybir.dt.uint8
+FP8X4 = mybir.dt.float8_e4m3fn_x4
+FP8 = mybir.dt.float8_e4m3fn
+ALU = mybir.AluOpType
+ACT = mybir.ActivationFunctionType
+
+P = 128
+NTOK = B * S
+NJ = D // P
+NG = K // 512
+NIT = NTOK // P
+LN_EPS = 1e-3
+Y_SCALE = 220.0
+
+SHARE0 = (
+    (("V", 0, 512), ("S", 512, 1024)),
+    (("V", 0, 512), ("S", 512, 1024)),
+)
+SHARE1 = (
+    (("S", 0, 512), ("G", 512, 768), ("G", 768, 1024)),
+    (("S", 0, 512), ("V", 512, 1024)),
+)
+SHARE = (
+    (("S", 0, 1024),),
+    (("S", 0, 192), ("V", 192, 256), ("G", 256, 512), ("G", 512, 768), ("G", 768, 1024)),
+)
+QW0 = (((0, 512), (512, 1024)), ((0, 512), (512, 1024)))
+QW1 = (((0, 512), (512, 1024)), ((0, 512), (512, 1024)))
+QW = (((0, 1024),), ((0, 256), (256, 768), (768, 1024)))
+HOLD = 2
+TAIL_G = 0
+
+
+def tile_multiheadattentionunit_pa_kernel(tc, attn, Wo, bo, query_inputs, gamma, beta, out_0, out_1):
+    nc = tc.nc
+    with ExitStack() as ctx:
+        const = ctx.enter_context(tc.tile_pool(name="const", bufs=1))
+        xpool = ctx.enter_context(tc.tile_pool(name="xpool", bufs=3))
+        wpool = ctx.enter_context(tc.tile_pool(name="wpool", bufs=6))
+        g0pool = ctx.enter_context(tc.tile_pool(name="g0pool", bufs=2))
+        g1pool = ctx.enter_context(tc.tile_pool(name="g1pool", bufs=1))
+        gapool = ctx.enter_context(tc.tile_pool(name="gapool", bufs=4))
+        cpool = ctx.enter_context(tc.tile_pool(name="cpool", bufs=2))
+        tailp = ctx.enter_context(tc.tile_pool(name="tailp", bufs=4))
+        stat = ctx.enter_context(tc.tile_pool(name="stat", bufs=4))
+        tpp = ctx.enter_context(tc.psum_pool(name="tpp", bufs=4))
+        mmp = ctx.enter_context(tc.psum_pool(name="mmp", bufs=4))
+        ctx.enter_context(tc.manual_schedule())
+
+        x_sb, w_raw, wg, ga, tp = {}, {}, {}, {}, {}
+        wc, wsc, ac, asc, mm = {}, {}, {}, {}, {}
+
+        def share(h):
+            return SHARE0 if h == 0 else (SHARE1 if h == 1 else SHARE)
+
+        def qw(h):
+            return QW0 if h == 0 else (QW1 if h == 1 else QW)
+
+        def load_a(h):
+            x_sb[h] = xpool.tile([P, NIT, K], BF16, name="x_sb", tag="x_sb")
+            for b in range(B):
+                nc.sync.dma_start(
+                    out=x_sb[h][:, 2 * b:2 * b + 2, :],
+                    in_=attn[b, h, :, :].rearrange("(i p) k -> p i k", p=P),
+                )
+
+        def load_w(h, g):
+            w_raw[h, g] = wpool.tile([P, 4, D], BF16, name="w_raw", tag="w_raw")
+            nc.sync.dma_start(
+                out=w_raw[h, g][:],
+                in_=Wo[h, 512 * g:512 * (g + 1), :].rearrange("(p t) d -> p t d", t=4),
+            )
+
+        def loads(h):
+            if h < H:
+                load_a(h)
+                load_w(h, 0)
+                load_w(h, 1)
+
+        def transposes(h):
+            for c in range(2):
+                for g in range(NG):
+                    tp[h, g, c] = tpp.tile([P, 2, 256], F32, name="tp", tag="tp")
+                    for i2 in range(2):
+                        words = x_sb[h][:, 2 * c + i2, :].bitcast(F32)
+                        for u in range(2):
+                            nc.tensor.transpose(
+                                tp[h, g, c][:, u, P * i2:P * (i2 + 1)],
+                                words[:, 256 * g + u:256 * (g + 1):2],
+                                ident_f[:],
+                            )
+
+        def copies_out(h):
+            for g in range(NG):
+                ga[h, g] = gapool.tile([P, 4 * NTOK], BF16, name="ga", tag="ga", align_bytes=64)
+            for c in range(2):
+                for g in range(NG):
+                    nc.scalar.copy(
+                        out=ga[h, g][:].bitcast(F32)[:, 512 * c:512 * (c + 1)].rearrange("p (n u) -> p n u", u=2),
+                        in_=tp[h, g, c][:].rearrange("p u n -> p n u"),
+                    )
+
+        def new_wg(h, g):
+            pool = g0pool if g == 0 else g1pool
+            wg[h, g] = pool.tile([P, D, 4], BF16, name="wg%d" % g, tag="wg%d" % g, align_bytes=64)
+
+        def interleave(h, g, who):
+            for eng, d0, d1 in share(h)[g]:
+                if eng != who:
+                    continue
+                dst = wg[h, g][:, d0:d1, :]
+                src = w_raw[h, g][:, :, d0:d1].rearrange("p t d -> p d t")
+                if eng == "S":
+                    nc.scalar.copy(out=dst, in_=src)
+                elif eng == "V":
+                    nc.vector.tensor_copy(out=dst, in_=src)
+                else:
+                    nc.gpsimd.tensor_scalar(out=dst, in0=src, scalar1=1.0, scalar2=0.0, op0=ALU.mult, op1=ALU.add)
+
+        def new_codes(h):
+            wc[h] = cpool.tile([P, NG, D], U32, name="wc", tag="wc", align_bytes=64)
+            wsc[h] = cpool.tile([P, NG, D], U8, name="wsc", tag="wsc", align_bytes=64)
+            ac[h] = cpool.tile([P, NG, NTOK], U32, name="ac", tag="ac", align_bytes=64)
+            asc[h] = cpool.tile([P, NG, NTOK], U8, name="asc", tag="asc", align_bytes=64)
+
+        def quant_w(h, g):
+            for d0, d1 in qw(h)[g]:
+                nc.vector.quantize_mx(
+                    out=wc[h][:, g, d0:d1].bitcast(FP8X4),
+                    scales=wsc[h][:, g, d0:d1],
+                    in_=wg[h, g][:, d0:d1, :].rearrange("p d t -> p (d t)"),
+                )
+
+        def quant_a(h):
+            for g in range(NG):
+                nc.vector.quantize_mx(
+                    out=ac[h][:, g, :].bitcast(FP8X4),
+                    scales=asc[h][:, g, :],
+                    in_=ga[h, g][:],
+                )
+
+        def matmuls(h, j):
+            mm[h, j] = mmp.tile([P, NTOK], F32, name="mm", tag="mm")
+            for g in range(NG):
+                nc.tensor.matmul_mx(
+                    out=mm[h, j][:],
+                    lhsT=wc[h][:, g, P * j:P * (j + 1)].bitcast(FP8X4),
+                    lhsT_scale=wsc[h][:, g, P * j:P * (j + 1)],
+                    rhs=ac[h][:, g, :].bitcast(FP8X4),
+                    rhs_scale=asc[h][:, g, :],
+                    start=(g == 0),
+                    stop=(g == NG - 1),
+                )
+
+        def epilogue(h, j):
+            col = NJ * h + j
+            if h == 0:
+                nc.vector.tensor_scalar(
+                    out=acc[j][:], in0=mm[h, j][:],
+                    scalar1=negb[:, col:col + 1], scalar2=negbsum[:, j:j + 1],
+                    op0=ALU.max, op1=ALU.subtract,
+                )
+            else:
+                nc.vector.scalar_tensor_tensor(
+                    out=acc[j][:], in0=mm[h, j][:], scalar=negb[:, col:col + 1], in1=acc[j][:],
+                    op0=ALU.max, op1=ALU.add,
+                )
+
+        ident_f = const.tile([P, P], F32, name="ident_f")
+        make_identity(nc, ident_f[:])
+        ident_b = const.tile([P, P], BF16, name="ident_b")
+        make_identity(nc, ident_b[:])
+        eps = const.tile([P, 1], F32, name="eps")
+        nc.vector.memset(eps[:], 1.0)
+        warm = const.tile([P, 1], F32, name="warm")
+        nc.scalar.activation(out=warm[:], in_=eps[:], func=ACT.Sqrt)
+        bo_rows = const.tile([P, P], BF16, name="bo_rows")
+        nc.vector.memset(bo_rows[:], 0.0)
+        acc = [const.tile([P, NTOK], F32, name="acc%d" % j) for j in range(NJ)]
+        q_sb = const.tile([P, NIT, D], BF16, name="q_sb")
+        g_bc = const.tile([P, D], BF16, name="g_bc")
+        b_bc = const.tile([P, D], BF16, name="b_bc")
+        negb = const.tile([P, H * NJ], F32, name="negb")
+        negbsum = const.tile([P, NJ], F32, name="negbsum")
+
+        nc.sync.dma_start(out=bo_rows[0:H * NJ, :], in_=bo.rearrange("h (j p) -> (h j) p", p=P))
+        loads(0)
+        loads(1)
+        loads(2)
+
+        bT = tpp.tile([P, P], BF16, name="bT", tag="tp")
+        nc.tensor.transpose(bT[:], bo_rows[:], ident_b[:])
+        nc.vector.tensor_scalar(out=negb[:], in0=bT[:, 0:H * NJ], scalar1=-1.0, scalar2=None, op0=ALU.mult)
+        nc.vector.tensor_reduce(
+            out=negbsum[:], in_=negb[:].rearrange("p (h j) -> p j h", h=H),
+            axis=mybir.AxisListType.X, op=ALU.add,
+        )
+        transposes(0)
+        copies_out(0)
+        new_wg(0, 0)
+        new_wg(0, 1)
+        new_codes(0)
+        interleave(0, 0, "V")
+        interleave(0, 0, "S")
+        quant_a(0)
+        quant_w(0, 0)
+        interleave(0, 1, "V")
+        interleave(0, 1, "S")
+        quant_w(0, 1)
+        loads(3)
+        transposes(1)
+        copies_out(1)
+        new_wg(1, 0)
+        interleave(1, 0, "S")
+        interleave(1, 0, "G")
+        new_wg(1, 1)
+        interleave(1, 1, "S")
+        interleave(1, 1, "G")
+
+        for s in range(H):
+            for j in range(NJ - HOLD):
+                matmuls(s, j)
+                epilogue(s, j)
+            for j in range(NJ - HOLD, NJ):
+                matmuls(s, j)
+            if s + 2 < H:
+                transposes(s + 2)
+                copies_out(s + 2)
+            if s + 1 < H:
+                n = s + 1
+                new_codes(n)
+                interleave(n, 0, "V")
+                interleave(n, 1, "V")
+                quant_w(n, 0)
+                quant_a(n)
+                quant_w(n, 1)
+            loads(s + 4)
+            if s + 2 < H:
+                n = s + 2
+                new_wg(n, 0)
+                new_wg(n, 1)
+                interleave(n, 1, "G")
+                interleave(n, 0, "S")
+                interleave(n, 1, "S")
+            for j in range(NJ - HOLD, NJ):
+                epilogue(s, j)
+            if s == 1:
+                for b in range(B):
+                    nc.sync.dma_start(
+                        out=q_sb[:, 2 * b:2 * b + 2, :],
+                        in_=query_inputs[b, :, :].rearrange("(i p) d -> p i d", p=P),
+                    )
+            if s == 2:
+                nc.sync.dma_start(out=g_bc[:], in_=gamma.partition_broadcast(P))
+                nc.sync.dma_start(out=b_bc[:], in_=beta.partition_broadcast(P))
+
+        xT = {}
+        for it in range(NIT):
+            for c in range(2):
+                pool = tpp if it < 2 else mmp
+                tag = "tp" if it < 2 else "mm"
+                xT[it, c] = pool.tile([P, 512], F32, name="xT", tag=tag)
+                nc.tensor.matmul(
+                    out=xT[it, c][:], lhsT=ident_b[:], rhs=q_sb[:, it, 512 * c:512 * (c + 1)],
+                    start=True, stop=False,
+                )
+                for jj in range(4):
+                    nc.tensor.matmul(
+                        out=xT[it, c][:, P * jj:P * (jj + 1)],
+                        lhsT=acc[4 * c + jj][:, P * it:P * (it + 1)],
+                        rhs=ident_f[:],
+                        is_transpose=True, start=False, stop=(jj == 3),
+                    )
+        mv, sd, rstd, tt = {}, {}, {}, {}
+
+        def stats(it):
+            st = stat.tile([P, 2, 6], F32, name="st", tag="st")
+            for c in range(2):
+                nc.vector.bn_stats(out=st[:, c, :], in_=xT[it, c][:])
+            mv[it] = stat.tile([P, 2], F32, name="mv", tag="mv")
+            nc.vector.bn_aggr(out=mv[it][:], in_=st[:].rearrange("p c s -> p (c s)"))
+            ve = stat.tile([P, 1], F32, name="ve", tag="ve")
+            nc.vector.tensor_scalar(out=ve[:], in0=mv[it][:, 1:2], scalar1=LN_EPS, scalar2=None, op0=ALU.add)
+            std = stat.tile([P, 1], F32, name="std", tag="std")
+            nc.scalar.activation(out=std[:], in_=ve[:], func=ACT.Sqrt)
+            sd[it] = std
+
+        def center(it):
+            tt[it] = tailp.tile([P, D], F32, name="t", tag="t")
+            for c in range(2):
+                nc.vector.scalar_tensor_tensor(
+                    out=tt[it][:, 512 * c:512 * (c + 1)], in0=xT[it, c][:], scalar=mv[it][:, 0:1],
+                    in1=g_bc[:, 512 * c:512 * (c + 1)], op0=ALU.subtract, op1=ALU.mult,
+                )
+
+        def finish(it):
+            b, i = it // 2, it % 2
+            o = tailp.tile([P, D], F32, name="o", tag="o")
+            o8 = tailp.tile([P, D], FP8, name="o8", tag="o8")
+            for c in range(2):
+                cols = slice(512 * c, 512 * (c + 1))
+                if it < TAIL_G:
+                    nc.scalar.activation(out=tt[it][:, cols], in_=tt[it][:, cols], func=ACT.Copy, scale=rstd[it][:])
+                    nc.gpsimd.tensor_tensor(out=o[:, cols], in0=tt[it][:, cols], in1=b_bc[:, cols], op=ALU.add)
+                else:
+                    nc.vector.scalar_tensor_tensor(
+                        out=o[:, cols], in0=tt[it][:, cols], scalar=rstd[it][:], in1=b_bc[:, cols],
+                        op0=ALU.mult, op1=ALU.add,
+                    )
+                nc.sync.dma_start(out=out_0[b, P * i:P * (i + 1), cols], in_=o[:, cols])
+            for c in range(2):
+                cols = slice(512 * c, 512 * (c + 1))
+                nc.scalar.activation(out=o8[:, cols], in_=o[:, cols], func=ACT.Copy, scale=Y_SCALE, saturate=False)
+            nc.sync.dma_start(out=out_1[b, P * i:P * (i + 1), :], in_=o8[:].bitcast(U8))
+
+        for it in range(NIT):
+            stats(it)
+        for it in range(NIT):
+            rstd[it] = stat.tile([P, 1], F32, name="rstd", tag="rstd")
+            nc.vector.reciprocal(out=rstd[it][:], in_=sd[it][:])
+        for it in range(TAIL_G):
+            center(it)
+        for it in range(TAIL_G):
+            finish(it)
+        for it in range(TAIL_G, NIT):
+            center(it)
+            finish(it)

@@ -38,8 +38,8 @@ SHARE = (
 QW0 = (((0, 512), (512, 1024)), ((0, 512), (512, 1024)))
 QW1 = (((0, 512), (512, 1024)), ((0, 512), (512, 1024)))
 QW = (((0, 1024),), ((0, 256), (256, 768), (768, 1024)))
+N_WARM = 4
 HOLD = 2
-TAIL_G = 0
 
 
 def tile_multiheadattentionunit_pa_kernel(tc, attn, Wo, bo, query_inputs, gamma, beta, out_0, out_1):
@@ -150,8 +150,14 @@ def tile_multiheadattentionunit_pa_kernel(tc, attn, Wo, bo, query_inputs, gamma,
                     in_=ga[h, g][:],
                 )
 
+        def warm_up(h):
+            mm[h, 0] = mmp.tile([P, NTOK], F32, name="mm", tag="mm")
+            for r in range(N_WARM):
+                nc.tensor.matmul(out=mm[h, 0][:], lhsT=ident_b[:], rhs=zeros[:], start=True, stop=True)
+
         def matmuls(h, j):
-            mm[h, j] = mmp.tile([P, NTOK], F32, name="mm", tag="mm")
+            if (h, j) not in mm:
+                mm[h, j] = mmp.tile([P, NTOK], F32, name="mm", tag="mm")
             for g in range(NG):
                 nc.tensor.matmul_mx(
                     out=mm[h, j][:],
@@ -177,6 +183,16 @@ def tile_multiheadattentionunit_pa_kernel(tc, attn, Wo, bo, query_inputs, gamma,
                     op0=ALU.max, op1=ALU.add,
                 )
 
+        xT = {}
+
+        def residual(it, pool, tag):
+            for c in range(2):
+                xT[it, c] = pool.tile([P, 512], F32, name="xT", tag=tag)
+                nc.tensor.matmul(
+                    out=xT[it, c][:], lhsT=ident_b[:], rhs=q_sb[:, it, 512 * c:512 * (c + 1)],
+                    start=True, stop=False,
+                )
+
         ident_f = const.tile([P, P], F32, name="ident_f")
         make_identity(nc, ident_f[:])
         ident_b = const.tile([P, P], BF16, name="ident_b")
@@ -185,6 +201,8 @@ def tile_multiheadattentionunit_pa_kernel(tc, attn, Wo, bo, query_inputs, gamma,
         nc.vector.memset(eps[:], 1.0)
         warm = const.tile([P, 1], F32, name="warm")
         nc.scalar.activation(out=warm[:], in_=eps[:], func=ACT.Sqrt)
+        zeros = const.tile([P, NTOK], BF16, name="zeros")
+        nc.vector.memset(zeros[:], 0.0)
         bo_rows = const.tile([P, P], BF16, name="bo_rows")
         nc.vector.memset(bo_rows[:], 0.0)
         acc = [const.tile([P, NTOK], F32, name="acc%d" % j) for j in range(NJ)]
@@ -194,18 +212,11 @@ def tile_multiheadattentionunit_pa_kernel(tc, attn, Wo, bo, query_inputs, gamma,
         negb = const.tile([P, H * NJ], F32, name="negb")
         negbsum = const.tile([P, NJ], F32, name="negbsum")
 
-        nc.sync.dma_start(out=bo_rows[0:H * NJ, :], in_=bo.rearrange("h (j p) -> (h j) p", p=P))
         loads(0)
+        nc.sync.dma_start(out=bo_rows[0:H * NJ, :], in_=bo.rearrange("h (j p) -> (h j) p", p=P))
         loads(1)
         loads(2)
 
-        bT = tpp.tile([P, P], BF16, name="bT", tag="tp")
-        nc.tensor.transpose(bT[:], bo_rows[:], ident_b[:])
-        nc.vector.tensor_scalar(out=negb[:], in0=bT[:, 0:H * NJ], scalar1=-1.0, scalar2=None, op0=ALU.mult)
-        nc.vector.tensor_reduce(
-            out=negbsum[:], in_=negb[:].rearrange("p (h j) -> p j h", h=H),
-            axis=mybir.AxisListType.X, op=ALU.add,
-        )
         transposes(0)
         copies_out(0)
         new_wg(0, 0)
@@ -217,6 +228,13 @@ def tile_multiheadattentionunit_pa_kernel(tc, attn, Wo, bo, query_inputs, gamma,
         quant_w(0, 0)
         interleave(0, 1, "V")
         interleave(0, 1, "S")
+        bT = tpp.tile([P, P], BF16, name="bT", tag="tp")
+        nc.tensor.transpose(bT[:], bo_rows[:], ident_b[:])
+        nc.vector.tensor_scalar(out=negb[:], in0=bT[:, 0:H * NJ], scalar1=-1.0, scalar2=None, op0=ALU.mult)
+        nc.vector.tensor_reduce(
+            out=negbsum[:], in_=negb[:].rearrange("p (h j) -> p j h", h=H),
+            axis=mybir.AxisListType.X, op=ALU.add,
+        )
         quant_w(0, 1)
         loads(3)
         transposes(1)
@@ -237,6 +255,11 @@ def tile_multiheadattentionunit_pa_kernel(tc, attn, Wo, bo, query_inputs, gamma,
             if s + 2 < H:
                 transposes(s + 2)
                 copies_out(s + 2)
+            if s + 2 == H:
+                residual(0, tpp, "tp")
+                residual(1, tpp, "tp")
+            if s + 1 < H:
+                warm_up(s + 1)
             if s + 1 < H:
                 n = s + 1
                 new_codes(n)
@@ -261,78 +284,141 @@ def tile_multiheadattentionunit_pa_kernel(tc, attn, Wo, bo, query_inputs, gamma,
                         out=q_sb[:, 2 * b:2 * b + 2, :],
                         in_=query_inputs[b, :, :].rearrange("(i p) d -> p i d", p=P),
                     )
-            if s == 2:
+            if s == 3:
                 nc.sync.dma_start(out=g_bc[:], in_=gamma.partition_broadcast(P))
                 nc.sync.dma_start(out=b_bc[:], in_=beta.partition_broadcast(P))
 
-        xT = {}
-        for it in range(NIT):
-            for c in range(2):
-                pool = tpp if it < 2 else mmp
-                tag = "tp" if it < 2 else "mm"
-                xT[it, c] = pool.tile([P, 512], F32, name="xT", tag=tag)
-                nc.tensor.matmul(
-                    out=xT[it, c][:], lhsT=ident_b[:], rhs=q_sb[:, it, 512 * c:512 * (c + 1)],
-                    start=True, stop=False,
-                )
-                for jj in range(4):
-                    nc.tensor.matmul(
-                        out=xT[it, c][:, P * jj:P * (jj + 1)],
-                        lhsT=acc[4 * c + jj][:, P * it:P * (it + 1)],
-                        rhs=ident_f[:],
-                        is_transpose=True, start=False, stop=(jj == 3),
-                    )
-        mv, sd, rstd, tt = {}, {}, {}, {}
+        def transposed(it, j):
+            nc.tensor.matmul(
+                out=xT[it, j // 4][:, P * (j % 4):P * (j % 4 + 1)],
+                lhsT=acc[j][:, P * it:P * (it + 1)],
+                rhs=ident_f[:],
+                is_transpose=True, start=False, stop=(j % 4 == 3),
+            )
 
-        def stats(it):
+        for j in range(NJ):
+            for it in range(2):
+                transposed(it, j)
+        for it in range(2, NIT):
+            residual(it, mmp, "mm")
+            for j in range(NJ):
+                transposed(it, j)
+
+        negmean, varsum, rstd, tt, sm, sq = {}, {}, {}, {}, {}, {}
+
+        def small(name):
+            return stat.tile([P, 1], F32, name=name, tag=name)
+
+        def stats_v(it):
             st = stat.tile([P, 2, 6], F32, name="st", tag="st")
             for c in range(2):
                 nc.vector.bn_stats(out=st[:, c, :], in_=xT[it, c][:])
-            mv[it] = stat.tile([P, 2], F32, name="mv", tag="mv")
-            nc.vector.bn_aggr(out=mv[it][:], in_=st[:].rearrange("p c s -> p (c s)"))
-            ve = stat.tile([P, 1], F32, name="ve", tag="ve")
-            nc.vector.tensor_scalar(out=ve[:], in0=mv[it][:, 1:2], scalar1=LN_EPS, scalar2=None, op0=ALU.add)
-            std = stat.tile([P, 1], F32, name="std", tag="std")
-            nc.scalar.activation(out=std[:], in_=ve[:], func=ACT.Sqrt)
-            sd[it] = std
+            mv = stat.tile([P, 2], F32, name="mv", tag="mv")
+            nc.vector.bn_aggr(out=mv[:], in_=st[:].rearrange("p c s -> p (c s)"))
+            negmean[it] = small("negmean")
+            nc.vector.tensor_scalar(out=negmean[it][:], in0=mv[:, 0:1], scalar1=-1.0, scalar2=None, op0=ALU.mult)
+            varsum[it] = small("varsum")
+            nc.vector.tensor_scalar(
+                out=varsum[it][:], in0=mv[:, 1:2], scalar1=float(D), scalar2=D * LN_EPS, op0=ALU.mult, op1=ALU.add,
+            )
 
-        def center(it):
-            tt[it] = tailp.tile([P, D], F32, name="t", tag="t")
+        def sum_s(it):
+            sm[it] = stat.tile([P, 2], F32, name="sm", tag="sm")
             for c in range(2):
-                nc.vector.scalar_tensor_tensor(
-                    out=tt[it][:, 512 * c:512 * (c + 1)], in0=xT[it, c][:], scalar=mv[it][:, 0:1],
-                    in1=g_bc[:, 512 * c:512 * (c + 1)], op0=ALU.subtract, op1=ALU.mult,
+                junk = tailp.tile([P, 512], F32, name="junk", tag="junk")
+                nc.scalar.activation(out=junk[:], in_=xT[it, c][:], func=ACT.Copy, accum_out=sm[it][:, c:c + 1])
+
+        def mean_v(it):
+            negmean[it] = small("negmean")
+            nc.vector.tensor_scalar(
+                out=negmean[it][:], in0=sm[it][:, 0:1], scalar1=sm[it][:, 1:2], scalar2=-1.0 / D,
+                op0=ALU.add, op1=ALU.mult,
+            )
+
+        def squares_s(it):
+            sq[it] = stat.tile([P, 2], F32, name="sq", tag="sq")
+            for c in range(2):
+                junk = tailp.tile([P, 512], F32, name="junk", tag="junk")
+                nc.scalar.activation(
+                    out=junk[:], in_=xT[it, c][:], func=ACT.Square, bias=negmean[it][:], accum_out=sq[it][:, c:c + 1],
                 )
 
-        def finish(it):
-            b, i = it // 2, it % 2
-            o = tailp.tile([P, D], F32, name="o", tag="o")
-            o8 = tailp.tile([P, D], FP8, name="o8", tag="o8")
-            for c in range(2):
-                cols = slice(512 * c, 512 * (c + 1))
-                if it < TAIL_G:
-                    nc.scalar.activation(out=tt[it][:, cols], in_=tt[it][:, cols], func=ACT.Copy, scale=rstd[it][:])
-                    nc.gpsimd.tensor_tensor(out=o[:, cols], in0=tt[it][:, cols], in1=b_bc[:, cols], op=ALU.add)
-                else:
-                    nc.vector.scalar_tensor_tensor(
-                        out=o[:, cols], in0=tt[it][:, cols], scalar=rstd[it][:], in1=b_bc[:, cols],
-                        op0=ALU.mult, op1=ALU.add,
-                    )
-                nc.sync.dma_start(out=out_0[b, P * i:P * (i + 1), cols], in_=o[:, cols])
-            for c in range(2):
-                cols = slice(512 * c, 512 * (c + 1))
-                nc.scalar.activation(out=o8[:, cols], in_=o[:, cols], func=ACT.Copy, scale=Y_SCALE, saturate=False)
-            nc.sync.dma_start(out=out_1[b, P * i:P * (i + 1), :], in_=o8[:].bitcast(U8))
+        def var_v(it):
+            varsum[it] = small("varsum")
+            nc.vector.tensor_scalar(
+                out=varsum[it][:], in0=sq[it][:, 0:1], scalar1=sq[it][:, 1:2], scalar2=D * LN_EPS,
+                op0=ALU.add, op1=ALU.add,
+            )
 
-        for it in range(NIT):
-            stats(it)
-        for it in range(NIT):
-            rstd[it] = stat.tile([P, 1], F32, name="rstd", tag="rstd")
-            nc.vector.reciprocal(out=rstd[it][:], in_=sd[it][:])
-        for it in range(TAIL_G):
-            center(it)
-        for it in range(TAIL_G):
-            finish(it)
-        for it in range(TAIL_G, NIT):
-            center(it)
-            finish(it)
+        def sqrt_s(it):
+            rstd[it] = small("std")
+            nc.scalar.activation(out=rstd[it][:], in_=varsum[it][:], func=ACT.Sqrt, scale=1.0 / D)
+
+        def recip_v(it):
+            std = rstd[it]
+            rstd[it] = small("rstd")
+            nc.vector.reciprocal(out=rstd[it][:], in_=std[:])
+
+        def center(it, c):
+            if c == 0:
+                tt[it] = tailp.tile([P, D], F32, name="t", tag="t")
+            nc.vector.scalar_tensor_tensor(
+                out=tt[it][:, 512 * c:512 * (c + 1)], in0=xT[it, c][:], scalar=negmean[it][:],
+                in1=g_bc[:, 512 * c:512 * (c + 1)], op0=ALU.add, op1=ALU.mult,
+            )
+
+        oo, o8 = {}, {}
+
+        def scale_shift(it):
+            b, i = it // 2, it % 2
+            oo[it] = tailp.tile([P, D], F32, name="o", tag="o")
+            for c in range(2):
+                cols = slice(512 * c, 512 * (c + 1))
+                nc.vector.scalar_tensor_tensor(
+                    out=oo[it][:, cols], in0=tt[it][:, cols], scalar=rstd[it][:], in1=b_bc[:, cols],
+                    op0=ALU.mult, op1=ALU.add,
+                )
+                nc.sync.dma_start(out=out_0[b, P * i:P * (i + 1), cols], in_=oo[it][:, cols])
+
+        def cast(it):
+            b, i = it // 2, it % 2
+            o8[it] = tailp.tile([P, D], FP8, name="o8", tag="o8")
+            for c in range(2):
+                cols = slice(512 * c, 512 * (c + 1))
+                nc.scalar.activation(out=o8[it][:, cols], in_=oo[it][:, cols], func=ACT.Copy, scale=Y_SCALE, saturate=False)
+            nc.sync.dma_start(out=out_1[b, P * i:P * (i + 1), :], in_=o8[it][:].bitcast(U8))
+
+        stats_v(0)
+        sum_s(2)
+        sqrt_s(0)
+        stats_v(1)
+        sqrt_s(1)
+        mean_v(2)
+        squares_s(2)
+        sum_s(3)
+        center(0, 0)
+        center(0, 1)
+        recip_v(0)
+        scale_shift(0)
+        var_v(2)
+        sqrt_s(2)
+        center(1, 0)
+        mean_v(3)
+        squares_s(3)
+        center(1, 1)
+        recip_v(1)
+        scale_shift(1)
+        cast(0)
+        var_v(3)
+        sqrt_s(3)
+        cast(1)
+        recip_v(2)
+        center(2, 0)
+        center(2, 1)
+        scale_shift(2)
+        cast(2)
+        recip_v(3)
+        center(3, 0)
+        center(3, 1)
+        scale_shift(3)
+        cast(3)

@@ -119,8 +119,8 @@ def tile_multiheadattentionunit_pa_kernel(tc, attn, Wo, bo, query_inputs, gamma,
             for eng, d0, d1 in share(h)[g]:
                 if eng != who:
                     continue
-                dst = wg[h, g][:, d0:d1, :]
-                src = w_raw[h, g][:, :, d0:d1].rearrange("p t d -> p d t")
+                dst = wg[h, g][:, d0:d1, :].rearrange("p (c i) t -> p c t i", i=4)
+                src = w_raw[h, g][:, :, d0:d1].rearrange("p t (c i) -> p c t i", i=4)
                 if eng == "S":
                     nc.scalar.copy(out=dst, in_=src)
                 elif eng == "V":

@@ -33,13 +33,13 @@ SHARE1 = (
 )
 SHARE = (
     (("S", 0, 1024),),
-    (("S", 0, 192), ("V", 192, 256), ("G", 256, 512), ("G", 512, 768), ("G", 768, 1024)),
+    (("S", 0, 256), ("G", 256, 640), ("G", 640, 1024)),
 )
 QW0 = (((0, 512), (512, 1024)), ((0, 512), (512, 1024)))
 QW1 = (((0, 512), (512, 1024)), ((0, 512), (512, 1024)))
-QW = (((0, 1024),), ((0, 256), (256, 768), (768, 1024)))
+QW = (((0, 1024),), ((0, 1024),))
 N_WARM = 4
-HOLD = 2
+HOLD = 3
 
 
 def tile_multiheadattentionunit_pa_kernel(tc, attn, Wo, bo, query_inputs, gamma, beta, out_0, out_1):
@@ -50,7 +50,7 @@ def tile_multiheadattentionunit_pa_kernel(tc, attn, Wo, bo, query_inputs, gamma,
         wpool = ctx.enter_context(tc.tile_pool(name="wpool", bufs=6))
         g0pool = ctx.enter_context(tc.tile_pool(name="g0pool", bufs=2))
         g1pool = ctx.enter_context(tc.tile_pool(name="g1pool", bufs=1))
-        gapool = ctx.enter_context(tc.tile_pool(name="gapool", bufs=4))
+        gapool = ctx.enter_context(tc.tile_pool(name="gapool", bufs=2))
         cpool = ctx.enter_context(tc.tile_pool(name="cpool", bufs=2))
         tailp = ctx.enter_context(tc.tile_pool(name="tailp", bufs=4))
         stat = ctx.enter_context(tc.tile_pool(name="stat", bufs=4))
@@ -102,12 +102,11 @@ def tile_multiheadattentionunit_pa_kernel(tc, attn, Wo, bo, query_inputs, gamma,
                             )
 
         def copies_out(h):
-            for g in range(NG):
-                ga[h, g] = gapool.tile([P, 4 * NTOK], BF16, name="ga", tag="ga", align_bytes=64)
+            ga[h] = gapool.tile([P, NG, 4 * NTOK], BF16, name="ga", tag="ga", align_bytes=64)
             for c in range(2):
                 for g in range(NG):
                     nc.scalar.copy(
-                        out=ga[h, g][:].bitcast(F32)[:, 512 * c:512 * (c + 1)].rearrange("p (n u) -> p n u", u=2),
+                        out=ga[h][:, g, :].bitcast(F32)[:, 512 * c:512 * (c + 1)].rearrange("p (n u) -> p n u", u=2),
                         in_=tp[h, g, c][:].rearrange("p u n -> p n u"),
                     )
 
@@ -143,12 +142,11 @@ def tile_multiheadattentionunit_pa_kernel(tc, attn, Wo, bo, query_inputs, gamma,
                 )
 
         def quant_a(h):
-            for g in range(NG):
-                nc.vector.quantize_mx(
-                    out=ac[h][:, g, :].bitcast(FP8X4),
-                    scales=asc[h][:, g, :],
-                    in_=ga[h, g][:],
-                )
+            nc.vector.quantize_mx(
+                out=ac[h][:].rearrange("p g n -> p (g n)").bitcast(FP8X4),
+                scales=asc[h][:].rearrange("p g n -> p (g n)"),
+                in_=ga[h][:].rearrange("p g n -> p (g n)"),
+            )
 
         def warm_up(h):
             mm[h, 0] = mmp.tile([P, NTOK], F32, name="mm", tag="mm")
@@ -369,11 +367,15 @@ def tile_multiheadattentionunit_pa_kernel(tc, attn, Wo, bo, query_inputs, gamma,
 
         oo, o8 = {}, {}
 
+        def pieces(it):
+            if it < NIT - 1:
+                return (slice(0, D),)
+            return (slice(0, D // 2), slice(D // 2, D))
+
         def scale_shift(it):
             b, i = it // 2, it % 2
             oo[it] = tailp.tile([P, D], F32, name="o", tag="o")
-            for c in range(2):
-                cols = slice(512 * c, 512 * (c + 1))
+            for cols in pieces(it):
                 nc.vector.scalar_tensor_tensor(
                     out=oo[it][:, cols], in0=tt[it][:, cols], scalar=rstd[it][:], in1=b_bc[:, cols],
                     op0=ALU.mult, op1=ALU.add,
@@ -383,8 +385,7 @@ def tile_multiheadattentionunit_pa_kernel(tc, attn, Wo, bo, query_inputs, gamma,
         def cast(it):
             b, i = it // 2, it % 2
             o8[it] = tailp.tile([P, D], FP8, name="o8", tag="o8")
-            for c in range(2):
-                cols = slice(512 * c, 512 * (c + 1))
+            for cols in pieces(it):
                 nc.scalar.activation(out=o8[it][:, cols], in_=oo[it][:, cols], func=ACT.Copy, scale=Y_SCALE, saturate=False)
             nc.sync.dma_start(out=out_1[b, P * i:P * (i + 1), :], in_=o8[it][:].bitcast(U8))
 

@@ -16,28 +16,25 @@ ALU = mybir.AluOpType
 ACT = mybir.ActivationFunctionType
 
 P = 128
+PACK = 4
+BANK = 512
 NTOK = B * S
 NJ = D // P
-NG = K // 512
+NG = K // (P * PACK)
 NIT = NTOK // P
 LN_EPS = 1e-3
 Y_SCALE = 220.0
 
-SHARE0 = (
-    (("V", 0, 512), ("S", 512, 1024)),
-    (("V", 0, 512), ("S", 512, 1024)),
-)
-SHARE1 = (
-    (("S", 0, 512), ("G", 512, 768), ("G", 768, 1024)),
-    (("S", 0, 512), ("V", 512, 1024)),
-)
-SHARE = (
-    (("S", 0, 1024),),
-    (("S", 0, 256), ("G", 256, 640), ("G", 640, 1024)),
-)
-QW0 = (((0, 512), (512, 1024)), ((0, 512), (512, 1024)))
-QW1 = (((0, 512), (512, 1024)), ((0, 512), (512, 1024)))
-QW = (((0, 1024),), ((0, 1024),))
+SHARES = {
+    0: ((("V", 0, 512), ("S", 512, 1024)), (("V", 0, 512), ("S", 512, 1024))),
+    1: ((("S", 0, 512), ("G", 512, 768), ("G", 768, 1024)), (("S", 0, 512), ("V", 512, 1024))),
+}
+SHARE = ((("S", 0, 1024),), (("S", 0, 256), ("G", 256, 640), ("G", 640, 1024)))
+CALLS = {
+    0: (((0, 512), (512, 1024)), ((0, 512), (512, 1024))),
+    1: (((0, 512), (512, 1024)), ((0, 512), (512, 1024))),
+}
+CALL = (((0, 1024),), ((0, 1024),))
 N_WARM = 4
 HOLD = 3
 
@@ -59,27 +56,27 @@ def tile_multiheadattentionunit_pa_kernel(tc, attn, Wo, bo, query_inputs, gamma,
         ctx.enter_context(tc.manual_schedule())
 
         x_sb, w_raw, wg, ga, tp = {}, {}, {}, {}, {}
-        wc, wsc, ac, asc, mm = {}, {}, {}, {}, {}
-
-        def share(h):
-            return SHARE0 if h == 0 else (SHARE1 if h == 1 else SHARE)
-
-        def qw(h):
-            return QW0 if h == 0 else (QW1 if h == 1 else QW)
+        wc, wsc, ac, asc, mm, xT = {}, {}, {}, {}, {}, {}
 
         def load_a(h):
             x_sb[h] = xpool.tile([P, NIT, K], BF16, name="x_sb", tag="x_sb")
-            for b in range(B):
+            if h < 2:
+                for b in range(B):
+                    nc.sync.dma_start(
+                        out=x_sb[h][:, 2 * b:2 * b + 2, :],
+                        in_=attn[b, h, :, :].rearrange("(p i) k -> p i k", i=2),
+                    )
+            else:
                 nc.sync.dma_start(
-                    out=x_sb[h][:, 2 * b:2 * b + 2, :],
-                    in_=attn[b, h, :, :].rearrange("(i p) k -> p i k", p=P),
+                    out=x_sb[h][:].rearrange("p (b i) k -> p b (i k)", b=B),
+                    in_=attn[:, h, :, :].rearrange("b (p i) k -> p b (i k)", i=2),
                 )
 
         def load_w(h, g):
-            w_raw[h, g] = wpool.tile([P, 4, D], BF16, name="w_raw", tag="w_raw")
+            w_raw[h, g] = wpool.tile([P, PACK, D], BF16, name="w_raw", tag="w_raw")
             nc.sync.dma_start(
                 out=w_raw[h, g][:],
-                in_=Wo[h, 512 * g:512 * (g + 1), :].rearrange("(p t) d -> p t d", t=4),
+                in_=Wo[h, 512 * g:512 * (g + 1), :].rearrange("(p t) d -> p t d", t=PACK),
             )
 
         def loads(h):
@@ -89,33 +86,33 @@ def tile_multiheadattentionunit_pa_kernel(tc, attn, Wo, bo, query_inputs, gamma,
                 load_w(h, 1)
 
         def transposes(h):
-            for c in range(2):
+            for b in range(B):
                 for g in range(NG):
-                    tp[h, g, c] = tpp.tile([P, 2, 256], F32, name="tp", tag="tp")
-                    for i2 in range(2):
-                        words = x_sb[h][:, 2 * c + i2, :].bitcast(F32)
+                    tp[h, g, b] = tpp.tile([P, 2, 2 * P], F32, name="tp", tag="tp")
+                    for i in range(2):
+                        words = x_sb[h][:, 2 * b + i, :].bitcast(F32)
                         for u in range(2):
                             nc.tensor.transpose(
-                                tp[h, g, c][:, u, P * i2:P * (i2 + 1)],
+                                tp[h, g, b][:, u, P * i:P * (i + 1)],
                                 words[:, 256 * g + u:256 * (g + 1):2],
                                 ident_f[:],
                             )
 
         def copies_out(h):
-            ga[h] = gapool.tile([P, NG, 4 * NTOK], BF16, name="ga", tag="ga", align_bytes=64)
-            for c in range(2):
+            ga[h] = gapool.tile([P, NG, PACK * NTOK], BF16, name="ga", tag="ga", align_bytes=64)
+            for b in range(B):
                 for g in range(NG):
                     nc.scalar.copy(
-                        out=ga[h][:, g, :].bitcast(F32)[:, 512 * c:512 * (c + 1)].rearrange("p (n u) -> p n u", u=2),
-                        in_=tp[h, g, c][:].rearrange("p u n -> p n u"),
+                        out=ga[h][:, g, :].bitcast(F32)[:, BANK * b:BANK * (b + 1)].rearrange("p (n u) -> p n u", u=2),
+                        in_=tp[h, g, b][:].rearrange("p u n -> p n u"),
                     )
 
         def new_wg(h, g):
             pool = g0pool if g == 0 else g1pool
-            wg[h, g] = pool.tile([P, D, 4], BF16, name="wg%d" % g, tag="wg%d" % g, align_bytes=64)
+            wg[h, g] = pool.tile([P, D, PACK], BF16, name="wg%d" % g, tag="wg%d" % g, align_bytes=64)
 
         def interleave(h, g, who):
-            for eng, d0, d1 in share(h)[g]:
+            for eng, d0, d1 in SHARES.get(h, SHARE)[g]:
                 if eng != who:
                     continue
                 dst = wg[h, g][:, d0:d1, :].rearrange("p (c i) t -> p c t i", i=4)
@@ -134,7 +131,7 @@ def tile_multiheadattentionunit_pa_kernel(tc, attn, Wo, bo, query_inputs, gamma,
             asc[h] = cpool.tile([P, NG, NTOK], U8, name="asc", tag="asc", align_bytes=64)
 
         def quant_w(h, g):
-            for d0, d1 in qw(h)[g]:
+            for d0, d1 in CALLS.get(h, CALL)[g]:
                 nc.vector.quantize_mx(
                     out=wc[h][:, g, d0:d1].bitcast(FP8X4),
                     scales=wsc[h][:, g, d0:d1],
@@ -181,28 +178,22 @@ def tile_multiheadattentionunit_pa_kernel(tc, attn, Wo, bo, query_inputs, gamma,
                     op0=ALU.max, op1=ALU.add,
                 )
 
-        xT = {}
-
-        def residual(it, pool, tag):
-            for c in range(2):
-                xT[it, c] = pool.tile([P, 512], F32, name="xT", tag=tag)
-                nc.tensor.matmul(
-                    out=xT[it, c][:], lhsT=ident_b[:], rhs=q_sb[:, it, 512 * c:512 * (c + 1)],
-                    start=True, stop=False,
-                )
-
         ident_f = const.tile([P, P], F32, name="ident_f")
         make_identity(nc, ident_f[:])
         ident_b = const.tile([P, P], BF16, name="ident_b")
         make_identity(nc, ident_b[:])
-        eps = const.tile([P, 1], F32, name="eps")
-        nc.vector.memset(eps[:], 1.0)
+        one = const.tile([P, 1], F32, name="one")
+        nc.vector.memset(one[:], 1.0)
         warm = const.tile([P, 1], F32, name="warm")
-        nc.scalar.activation(out=warm[:], in_=eps[:], func=ACT.Sqrt)
+        nc.scalar.activation(out=warm[:], in_=one[:], func=ACT.Sqrt)
         zeros = const.tile([P, NTOK], BF16, name="zeros")
         nc.vector.memset(zeros[:], 0.0)
         bo_rows = const.tile([P, P], BF16, name="bo_rows")
         nc.vector.memset(bo_rows[:], 0.0)
+        g_row = const.tile([P, D], BF16, name="g_row")
+        nc.vector.memset(g_row[:], 0.0)
+        b_row = const.tile([P, D], BF16, name="b_row")
+        nc.vector.memset(b_row[:], 0.0)
         acc = [const.tile([P, NTOK], F32, name="acc%d" % j) for j in range(NJ)]
         q_sb = const.tile([P, NIT, D], BF16, name="q_sb")
         g_bc = const.tile([P, D], BF16, name="g_bc")
@@ -214,6 +205,8 @@ def tile_multiheadattentionunit_pa_kernel(tc, attn, Wo, bo, query_inputs, gamma,
         nc.sync.dma_start(out=bo_rows[0:H * NJ, :], in_=bo.rearrange("h (j p) -> (h j) p", p=P))
         loads(1)
         loads(2)
+        nc.sync.dma_start(out=g_row[0:1, :], in_=gamma.rearrange("(o d) -> o d", o=1))
+        nc.sync.dma_start(out=b_row[0:1, :], in_=beta.rearrange("(o d) -> o d", o=1))
 
         transposes(0)
         copies_out(0)
@@ -254,37 +247,44 @@ def tile_multiheadattentionunit_pa_kernel(tc, attn, Wo, bo, query_inputs, gamma,
                 transposes(s + 2)
                 copies_out(s + 2)
             if s + 2 == H:
-                residual(0, tpp, "tp")
-                residual(1, tpp, "tp")
+                for row, spread in ((g_row, g_bc), (b_row, b_bc)):
+                    for c in range(D // BANK):
+                        picked = tpp.tile([P, BANK], F32, name="picked", tag="tp")
+                        nc.tensor.matmul(
+                            out=picked[:], lhsT=ident_b[:, 0:1].to_broadcast([P, P]),
+                            rhs=row[:, BANK * c:BANK * (c + 1)], start=True, stop=True,
+                        )
+                        nc.scalar.copy(out=spread[:, BANK * c:BANK * (c + 1)], in_=picked[:])
             if s + 1 < H:
                 warm_up(s + 1)
-            if s + 1 < H:
-                n = s + 1
-                new_codes(n)
-                interleave(n, 0, "V")
-                interleave(n, 1, "V")
-                quant_w(n, 0)
-                quant_a(n)
-                quant_w(n, 1)
+                new_codes(s + 1)
+                interleave(s + 1, 0, "V")
+                interleave(s + 1, 1, "V")
+                quant_a(s + 1)
+                quant_w(s + 1, 0)
+                quant_w(s + 1, 1)
             loads(s + 4)
+            if s + 4 == H:
+                nc.sync.dma_start(
+                    out=q_sb[:].rearrange("p (b i) d -> p b (i d)", b=B),
+                    in_=query_inputs.rearrange("b (p i) d -> p b (i d)", i=2),
+                )
             if s + 2 < H:
-                n = s + 2
-                new_wg(n, 0)
-                new_wg(n, 1)
-                interleave(n, 1, "G")
-                interleave(n, 0, "S")
-                interleave(n, 1, "S")
+                new_wg(s + 2, 0)
+                new_wg(s + 2, 1)
+                interleave(s + 2, 1, "G")
+                interleave(s + 2, 0, "S")
+                interleave(s + 2, 1, "S")
             for j in range(NJ - HOLD, NJ):
                 epilogue(s, j)
-            if s == 1:
-                for b in range(B):
-                    nc.sync.dma_start(
-                        out=q_sb[:, 2 * b:2 * b + 2, :],
-                        in_=query_inputs[b, :, :].rearrange("(i p) d -> p i d", p=P),
-                    )
-            if s == 3:
-                nc.sync.dma_start(out=g_bc[:], in_=gamma.partition_broadcast(P))
-                nc.sync.dma_start(out=b_bc[:], in_=beta.partition_broadcast(P))
+
+        def residual(it, pool, tag):
+            for c in range(D // BANK):
+                xT[it, c] = pool.tile([P, BANK], F32, name="xT", tag=tag)
+                nc.tensor.matmul(
+                    out=xT[it, c][:], lhsT=ident_b[:], rhs=q_sb[:, it, BANK * c:BANK * (c + 1)],
+                    start=True, stop=False,
+                )
 
         def transposed(it, j):
             nc.tensor.matmul(
@@ -294,6 +294,8 @@ def tile_multiheadattentionunit_pa_kernel(tc, attn, Wo, bo, query_inputs, gamma,
                 is_transpose=True, start=False, stop=(j % 4 == 3),
             )
 
+        residual(0, tpp, "tp")
+        residual(1, tpp, "tp")
         for j in range(NJ):
             for it in range(2):
                 transposed(it, j)
@@ -302,7 +304,7 @@ def tile_multiheadattentionunit_pa_kernel(tc, attn, Wo, bo, query_inputs, gamma,
             for j in range(NJ):
                 transposed(it, j)
 
-        negmean, varsum, rstd, tt, sm, sq = {}, {}, {}, {}, {}, {}
+        negmean, varsum, std, rstd, centred, result, codes8, sums, squares = {}, {}, {}, {}, {}, {}, {}, {}, {}
 
         def small(name):
             return stat.tile([P, 1], F32, name=name, tag=name)
@@ -321,73 +323,74 @@ def tile_multiheadattentionunit_pa_kernel(tc, attn, Wo, bo, query_inputs, gamma,
             )
 
         def sum_s(it):
-            sm[it] = stat.tile([P, 2], F32, name="sm", tag="sm")
+            sums[it] = stat.tile([P, 2], F32, name="sm", tag="sm")
             for c in range(2):
-                junk = tailp.tile([P, 512], F32, name="junk", tag="junk")
-                nc.scalar.activation(out=junk[:], in_=xT[it, c][:], func=ACT.Copy, accum_out=sm[it][:, c:c + 1])
+                junk = tailp.tile([P, BANK], F32, name="junk", tag="junk")
+                nc.scalar.activation(out=junk[:], in_=xT[it, c][:], func=ACT.Copy, accum_out=sums[it][:, c:c + 1])
 
         def mean_v(it):
             negmean[it] = small("negmean")
             nc.vector.tensor_scalar(
-                out=negmean[it][:], in0=sm[it][:, 0:1], scalar1=sm[it][:, 1:2], scalar2=-1.0 / D,
+                out=negmean[it][:], in0=sums[it][:, 0:1], scalar1=sums[it][:, 1:2], scalar2=-1.0 / D,
                 op0=ALU.add, op1=ALU.mult,
             )
 
         def squares_s(it):
-            sq[it] = stat.tile([P, 2], F32, name="sq", tag="sq")
+            squares[it] = stat.tile([P, 2], F32, name="sq", tag="sq")
             for c in range(2):
-                junk = tailp.tile([P, 512], F32, name="junk", tag="junk")
+                junk = tailp.tile([P, BANK], F32, name="junk", tag="junk")
                 nc.scalar.activation(
-                    out=junk[:], in_=xT[it, c][:], func=ACT.Square, bias=negmean[it][:], accum_out=sq[it][:, c:c + 1],
+                    out=junk[:], in_=xT[it, c][:], func=ACT.Square, bias=negmean[it][:],
+                    accum_out=squares[it][:, c:c + 1],
                 )
 
         def var_v(it):
             varsum[it] = small("varsum")
             nc.vector.tensor_scalar(
-                out=varsum[it][:], in0=sq[it][:, 0:1], scalar1=sq[it][:, 1:2], scalar2=D * LN_EPS,
+                out=varsum[it][:], in0=squares[it][:, 0:1], scalar1=squares[it][:, 1:2], scalar2=D * LN_EPS,
                 op0=ALU.add, op1=ALU.add,
             )
 
         def sqrt_s(it):
-            rstd[it] = small("std")
-            nc.scalar.activation(out=rstd[it][:], in_=varsum[it][:], func=ACT.Sqrt, scale=1.0 / D)
+            std[it] = small("std")
+            nc.scalar.activation(out=std[it][:], in_=varsum[it][:], func=ACT.Sqrt, scale=1.0 / D)
 
         def recip_v(it):
-            std = rstd[it]
             rstd[it] = small("rstd")
-            nc.vector.reciprocal(out=rstd[it][:], in_=std[:])
+            nc.vector.reciprocal(out=rstd[it][:], in_=std[it][:])
 
         def center(it, c):
             if c == 0:
-                tt[it] = tailp.tile([P, D], F32, name="t", tag="t")
+                centred[it] = tailp.tile([P, D], F32, name="t", tag="t")
             nc.vector.scalar_tensor_tensor(
-                out=tt[it][:, 512 * c:512 * (c + 1)], in0=xT[it, c][:], scalar=negmean[it][:],
-                in1=g_bc[:, 512 * c:512 * (c + 1)], op0=ALU.add, op1=ALU.mult,
+                out=centred[it][:, BANK * c:BANK * (c + 1)], in0=xT[it, c][:], scalar=negmean[it][:],
+                in1=g_bc[:, BANK * c:BANK * (c + 1)], op0=ALU.add, op1=ALU.mult,
             )
-
-        oo, o8 = {}, {}
 
         def pieces(it):
             if it < NIT - 1:
                 return (slice(0, D),)
             return (slice(0, D // 2), slice(D // 2, D))
 
+        def rows(out, it):
+            return out[it // 2, :, :].rearrange("(p i) d -> p i d", i=2)[:, it % 2, :]
+
         def scale_shift(it):
-            b, i = it // 2, it % 2
-            oo[it] = tailp.tile([P, D], F32, name="o", tag="o")
+            result[it] = tailp.tile([P, D], F32, name="o", tag="o")
             for cols in pieces(it):
                 nc.vector.scalar_tensor_tensor(
-                    out=oo[it][:, cols], in0=tt[it][:, cols], scalar=rstd[it][:], in1=b_bc[:, cols],
+                    out=result[it][:, cols], in0=centred[it][:, cols], scalar=rstd[it][:], in1=b_bc[:, cols],
                     op0=ALU.mult, op1=ALU.add,
                 )
-                nc.sync.dma_start(out=out_0[b, P * i:P * (i + 1), cols], in_=oo[it][:, cols])
+                nc.sync.dma_start(out=rows(out_0, it)[:, cols], in_=result[it][:, cols])
 
         def cast(it):
-            b, i = it // 2, it % 2
-            o8[it] = tailp.tile([P, D], FP8, name="o8", tag="o8")
+            codes8[it] = tailp.tile([P, D], FP8, name="o8", tag="o8")
             for cols in pieces(it):
-                nc.scalar.activation(out=o8[it][:, cols], in_=oo[it][:, cols], func=ACT.Copy, scale=Y_SCALE, saturate=False)
-            nc.sync.dma_start(out=out_1[b, P * i:P * (i + 1), :], in_=o8[it][:].bitcast(U8))
+                nc.scalar.activation(
+                    out=codes8[it][:, cols], in_=result[it][:, cols], func=ACT.Copy, scale=Y_SCALE, saturate=False,
+                )
+            nc.sync.dma_start(out=rows(out_1, it), in_=codes8[it][:].bitcast(U8))
 
         stats_v(0)
         sum_s(2)

@@ -33,10 +33,13 @@ SHARE = ((("S", 0, 1024),), (("S", 0, 256), ("G", 256, 640), ("G", 640, 1024)))
 CALLS = {
     0: (((0, 512), (512, 1024)), ((0, 512), (512, 1024))),
     1: (((0, 512), (512, 1024)), ((0, 512), (512, 1024))),
+    7: (((0, 512), (512, 1024)), ((0, 512), (512, 1024))),
 }
 CALL = (((0, 1024),), ((0, 1024),))
 N_WARM = 4
 HOLD = 3
+S_RUNS = ((6, 5, 8), (7, 0, 2))
+S_SET = frozenset((h, j) for h, j0, j1 in S_RUNS for j in range(j0, j1))
 
 
 def tile_multiheadattentionunit_pa_kernel(tc, attn, Wo, bo, query_inputs, gamma, beta, out_0, out_1):
@@ -85,8 +88,8 @@ def tile_multiheadattentionunit_pa_kernel(tc, attn, Wo, bo, query_inputs, gamma,
                 load_w(h, 0)
                 load_w(h, 1)
 
-        def transposes(h):
-            for b in range(B):
+        def transposes(h, batches=(0, 1)):
+            for b in batches:
                 for g in range(NG):
                     tp[h, g, b] = tpp.tile([P, 2, 2 * P], F32, name="tp", tag="tp")
                     for i in range(2):
@@ -98,9 +101,10 @@ def tile_multiheadattentionunit_pa_kernel(tc, attn, Wo, bo, query_inputs, gamma,
                                 ident_f[:],
                             )
 
-        def copies_out(h):
-            ga[h] = gapool.tile([P, NG, PACK * NTOK], BF16, name="ga", tag="ga", align_bytes=64)
-            for b in range(B):
+        def copies_out(h, batches=(0, 1)):
+            if h not in ga:
+                ga[h] = gapool.tile([P, NG, PACK * NTOK], BF16, name="ga", tag="ga", align_bytes=64)
+            for b in batches:
                 for g in range(NG):
                     nc.scalar.copy(
                         out=ga[h][:, g, :].bitcast(F32)[:, BANK * b:BANK * (b + 1)].rearrange("p (n u) -> p n u", u=2),
@@ -130,8 +134,8 @@ def tile_multiheadattentionunit_pa_kernel(tc, attn, Wo, bo, query_inputs, gamma,
             ac[h] = cpool.tile([P, NG, NTOK], U32, name="ac", tag="ac", align_bytes=64)
             asc[h] = cpool.tile([P, NG, NTOK], U8, name="asc", tag="asc", align_bytes=64)
 
-        def quant_w(h, g):
-            for d0, d1 in CALLS.get(h, CALL)[g]:
+        def quant_w(h, g, parts=slice(None)):
+            for d0, d1 in CALLS.get(h, CALL)[g][parts]:
                 nc.vector.quantize_mx(
                     out=wc[h][:, g, d0:d1].bitcast(FP8X4),
                     scales=wsc[h][:, g, d0:d1],
@@ -166,7 +170,10 @@ def tile_multiheadattentionunit_pa_kernel(tc, attn, Wo, bo, query_inputs, gamma,
 
         def epilogue(h, j):
             col = NJ * h + j
-            if h == 0:
+            if (h, j) in S_SET:
+                r_sb[h, j] = const.tile([P, NTOK], F32, name="r_sb%d_%d" % (h, j))
+                nc.scalar.activation(out=r_sb[h, j][:], in_=mm[h, j][:], func=ACT.Relu, bias=posb[:, col:col + 1])
+            elif h == min(hh for hh in range(H) if (hh, j) not in S_SET):
                 nc.vector.tensor_scalar(
                     out=acc[j][:], in0=mm[h, j][:],
                     scalar1=negb[:, col:col + 1], scalar2=negbsum[:, j:j + 1],
@@ -190,23 +197,19 @@ def tile_multiheadattentionunit_pa_kernel(tc, attn, Wo, bo, query_inputs, gamma,
         nc.vector.memset(zeros[:], 0.0)
         bo_rows = const.tile([P, P], BF16, name="bo_rows")
         nc.vector.memset(bo_rows[:], 0.0)
-        g_row = const.tile([P, D], BF16, name="g_row")
-        nc.vector.memset(g_row[:], 0.0)
-        b_row = const.tile([P, D], BF16, name="b_row")
-        nc.vector.memset(b_row[:], 0.0)
         acc = [const.tile([P, NTOK], F32, name="acc%d" % j) for j in range(NJ)]
         q_sb = const.tile([P, NIT, D], BF16, name="q_sb")
         g_bc = const.tile([P, D], BF16, name="g_bc")
         b_bc = const.tile([P, D], BF16, name="b_bc")
         negb = const.tile([P, H * NJ], F32, name="negb")
         negbsum = const.tile([P, NJ], F32, name="negbsum")
+        posb = const.tile([P, H * NJ], F32, name="posb")
+        r_sb = {}
 
         loads(0)
         nc.sync.dma_start(out=bo_rows[0:H * NJ, :], in_=bo.rearrange("h (j p) -> (h j) p", p=P))
         loads(1)
         loads(2)
-        nc.sync.dma_start(out=g_row[0:1, :], in_=gamma.rearrange("(o d) -> o d", o=1))
-        nc.sync.dma_start(out=b_row[0:1, :], in_=beta.rearrange("(o d) -> o d", o=1))
 
         transposes(0)
         copies_out(0)
@@ -219,14 +222,19 @@ def tile_multiheadattentionunit_pa_kernel(tc, attn, Wo, bo, query_inputs, gamma,
         quant_w(0, 0)
         interleave(0, 1, "V")
         interleave(0, 1, "S")
-        bT = tpp.tile([P, P], BF16, name="bT", tag="tp")
+        quant_w(0, 1)
+        bT = mmp.tile([P, P], BF16, name="bT", tag="mm")
         nc.tensor.transpose(bT[:], bo_rows[:], ident_b[:])
         nc.vector.tensor_scalar(out=negb[:], in0=bT[:, 0:H * NJ], scalar1=-1.0, scalar2=None, op0=ALU.mult)
+        nc.vector.tensor_copy(out=posb[:], in_=bT[:, 0:H * NJ])
         nc.vector.tensor_reduce(
             out=negbsum[:], in_=negb[:].rearrange("p (h j) -> p j h", h=H),
             axis=mybir.AxisListType.X, op=ALU.add,
         )
-        quant_w(0, 1)
+        for h, j0, j1 in S_RUNS:
+            nc.vector.tensor_tensor(
+                out=negbsum[:, j0:j1], in0=negbsum[:, j0:j1], in1=posb[:, NJ * h + j0:NJ * h + j1], op=ALU.add,
+            )
         loads(3)
         transposes(1)
         copies_out(1)
@@ -237,44 +245,35 @@ def tile_multiheadattentionunit_pa_kernel(tc, attn, Wo, bo, query_inputs, gamma,
         interleave(1, 1, "S")
         interleave(1, 1, "G")
 
-        for s in range(H):
+        for s in range(H - 2):
             for j in range(NJ - HOLD):
                 matmuls(s, j)
                 epilogue(s, j)
             for j in range(NJ - HOLD, NJ):
                 matmuls(s, j)
-            if s + 2 < H:
-                transposes(s + 2)
-                copies_out(s + 2)
-            if s + 2 == H:
-                for row, spread in ((g_row, g_bc), (b_row, b_bc)):
-                    for c in range(D // BANK):
-                        picked = tpp.tile([P, BANK], F32, name="picked", tag="tp")
-                        nc.tensor.matmul(
-                            out=picked[:], lhsT=ident_b[:, 0:1].to_broadcast([P, P]),
-                            rhs=row[:, BANK * c:BANK * (c + 1)], start=True, stop=True,
-                        )
-                        nc.scalar.copy(out=spread[:, BANK * c:BANK * (c + 1)], in_=picked[:])
-            if s + 1 < H:
-                warm_up(s + 1)
-                new_codes(s + 1)
-                interleave(s + 1, 0, "V")
-                interleave(s + 1, 1, "V")
-                quant_a(s + 1)
-                quant_w(s + 1, 0)
-                quant_w(s + 1, 1)
+            transposes(s + 2)
+            copies_out(s + 2)
+            warm_up(s + 1)
+            new_codes(s + 1)
+            interleave(s + 1, 0, "V")
+            interleave(s + 1, 1, "V")
+            quant_a(s + 1)
+            quant_w(s + 1, 0)
+            quant_w(s + 1, 1)
             loads(s + 4)
             if s + 4 == H:
                 nc.sync.dma_start(
                     out=q_sb[:].rearrange("p (b i) d -> p b (i d)", b=B),
                     in_=query_inputs.rearrange("b (p i) d -> p b (i d)", i=2),
                 )
-            if s + 2 < H:
-                new_wg(s + 2, 0)
-                new_wg(s + 2, 1)
-                interleave(s + 2, 1, "G")
-                interleave(s + 2, 0, "S")
-                interleave(s + 2, 1, "S")
+            if s + 3 == H:
+                nc.sync.dma_start(out=g_bc[:], in_=gamma.partition_broadcast(P))
+                nc.sync.dma_start(out=b_bc[:], in_=beta.partition_broadcast(P))
+            new_wg(s + 2, 0)
+            new_wg(s + 2, 1)
+            interleave(s + 2, 1, "G")
+            interleave(s + 2, 0, "S")
+            interleave(s + 2, 1, "S")
             for j in range(NJ - HOLD, NJ):
                 epilogue(s, j)
 
@@ -286,23 +285,45 @@ def tile_multiheadattentionunit_pa_kernel(tc, attn, Wo, bo, query_inputs, gamma,
                     start=True, stop=False,
                 )
 
-        def transposed(it, j):
-            nc.tensor.matmul(
-                out=xT[it, j // 4][:, P * (j % 4):P * (j % 4 + 1)],
-                lhsT=acc[j][:, P * it:P * (it + 1)],
-                rhs=ident_f[:],
-                is_transpose=True, start=False, stop=(j % 4 == 3),
-            )
+        def transposed(it, j, srcs, close):
+            for n, t_ in enumerate(srcs):
+                nc.tensor.matmul(
+                    out=xT[it, j // 4][:, P * (j % 4):P * (j % 4 + 1)],
+                    lhsT=t_[:, P * it:P * (it + 1)],
+                    rhs=ident_f[:],
+                    is_transpose=True, start=False, stop=(close and n == len(srcs) - 1),
+                )
 
+        LAST = H - 1
+        for j in range(NJ - HOLD):
+            matmuls(LAST - 1, j)
+            epilogue(LAST - 1, j)
+        for j in range(NJ - HOLD, NJ):
+            matmuls(LAST - 1, j)
         residual(0, tpp, "tp")
         residual(1, tpp, "tp")
-        for j in range(NJ):
+        new_codes(LAST)
+        quant_a(LAST)
+        for half in range(2):
+            for g in range(NG):
+                quant_w(LAST, g, slice(half, half + 1))
+        for j in range(NJ - HOLD, NJ):
+            epilogue(LAST - 1, j)
+        early = [j for j in range(NJ) if (LAST, j) in S_SET]
+        for j in early:
             for it in range(2):
-                transposed(it, j)
-        for it in range(2, NIT):
-            residual(it, mmp, "mm")
+                transposed(it, j, [acc[j]], False)
+        for j in range(NJ):
+            matmuls(LAST, j)
+            epilogue(LAST, j)
+        for it in range(NIT):
+            if it >= 2:
+                residual(it, mmp, "mm")
             for j in range(NJ):
-                transposed(it, j)
+                srcs = [r_sb[h, j] for h in range(H) if (h, j) in S_SET]
+                if it >= 2 or j not in early:
+                    srcs.append(acc[j])
+                transposed(it, j, srcs, j % 4 == 3)
 
         negmean, varsum, std, rstd, centred, result, codes8, sums, squares = {}, {}, {}, {}, {}, {}, {}, {}, {}
 
@@ -386,43 +407,49 @@ def tile_multiheadattentionunit_pa_kernel(tc, attn, Wo, bo, query_inputs, gamma,
 
         def cast(it):
             codes8[it] = tailp.tile([P, D], FP8, name="o8", tag="o8")
-            for cols in pieces(it):
-                nc.scalar.activation(
-                    out=codes8[it][:, cols], in_=result[it][:, cols], func=ACT.Copy, scale=Y_SCALE, saturate=False,
-                )
+            for n, cols in enumerate(pieces(it)):
+                if n == 1:
+                    nc.vector.tensor_scalar(
+                        out=codes8[it][:, cols], in0=result[it][:, cols], scalar1=Y_SCALE, scalar2=None, op0=ALU.mult,
+                        saturate=False,
+                    )
+                else:
+                    nc.scalar.activation(
+                        out=codes8[it][:, cols], in_=result[it][:, cols], func=ACT.Copy, scale=Y_SCALE, saturate=False,
+                    )
             nc.sync.dma_start(out=rows(out_1, it), in_=codes8[it][:].bitcast(U8))
 
         stats_v(0)
-        sum_s(2)
+        sum_s(1)
         sqrt_s(0)
-        stats_v(1)
-        sqrt_s(1)
-        mean_v(2)
-        squares_s(2)
-        sum_s(3)
         center(0, 0)
         center(0, 1)
+        mean_v(1)
+        squares_s(1)
         recip_v(0)
         scale_shift(0)
-        var_v(2)
+        cast(0)
+        stats_v(2)
+        var_v(1)
+        sqrt_s(1)
         sqrt_s(2)
         center(1, 0)
-        mean_v(3)
-        squares_s(3)
         center(1, 1)
         recip_v(1)
+        sum_s(3)
         scale_shift(1)
-        cast(0)
-        var_v(3)
-        sqrt_s(3)
-        cast(1)
+        mean_v(3)
+        squares_s(3)
         recip_v(2)
         center(2, 0)
         center(2, 1)
+        cast(1)
         scale_shift(2)
+        var_v(3)
+        sqrt_s(3)
         cast(2)
-        recip_v(3)
         center(3, 0)
         center(3, 1)
+        recip_v(3)
         scale_shift(3)
         cast(3)

@@ -192,7 +192,7 @@ def tile_multiheadattentionunit_pa_kernel(tc, attn, Wo, bo, query_inputs, gamma,
         one = const.tile([P, 1], F32, name="one")
         nc.vector.memset(one[:], 1.0)
         warm = const.tile([P, 1], F32, name="warm")
-        nc.scalar.activation(out=warm[:], in_=one[:], func=ACT.Sqrt)
+        nc.scalar.activation(out=warm[:], in_=one[:], func=ACT.Abs_reciprocal_sqrt)
         zeros = const.tile([P, NTOK], BF16, name="zeros")
         nc.vector.memset(zeros[:], 0.0)
         bo_rows = const.tile([P, P], BF16, name="bo_rows")
@@ -325,7 +325,7 @@ def tile_multiheadattentionunit_pa_kernel(tc, attn, Wo, bo, query_inputs, gamma,
                     srcs.append(acc[j])
                 transposed(it, j, srcs, j % 4 == 3)
 
-        negmean, varsum, std, rstd, centred, result, codes8, sums, squares = {}, {}, {}, {}, {}, {}, {}, {}, {}
+        mean, negmean, varsum, rstd, centred, result, codes8, sums, squares = {}, {}, {}, {}, {}, {}, {}, {}, {}
 
         def small(name):
             return stat.tile([P, 1], F32, name=name, tag=name)
@@ -336,8 +336,7 @@ def tile_multiheadattentionunit_pa_kernel(tc, attn, Wo, bo, query_inputs, gamma,
                 nc.vector.bn_stats(out=st[:, c, :], in_=xT[it, c][:])
             mv = stat.tile([P, 2], F32, name="mv", tag="mv")
             nc.vector.bn_aggr(out=mv[:], in_=st[:].rearrange("p c s -> p (c s)"))
-            negmean[it] = small("negmean")
-            nc.vector.tensor_scalar(out=negmean[it][:], in0=mv[:, 0:1], scalar1=-1.0, scalar2=None, op0=ALU.mult)
+            mean[it] = mv
             varsum[it] = small("varsum")
             nc.vector.tensor_scalar(
                 out=varsum[it][:], in0=mv[:, 1:2], scalar1=float(D), scalar2=D * LN_EPS, op0=ALU.mult, op1=ALU.add,
@@ -349,9 +348,9 @@ def tile_multiheadattentionunit_pa_kernel(tc, attn, Wo, bo, query_inputs, gamma,
                 junk = tailp.tile([P, BANK], F32, name="junk", tag="junk")
                 nc.scalar.activation(out=junk[:], in_=xT[it, c][:], func=ACT.Copy, accum_out=sums[it][:, c:c + 1])
 
-        def mean_v(it):
+        def mean_g(it):
             negmean[it] = small("negmean")
-            nc.vector.tensor_scalar(
+            nc.gpsimd.tensor_scalar(
                 out=negmean[it][:], in0=sums[it][:, 0:1], scalar1=sums[it][:, 1:2], scalar2=-1.0 / D,
                 op0=ALU.add, op1=ALU.mult,
             )
@@ -365,27 +364,27 @@ def tile_multiheadattentionunit_pa_kernel(tc, attn, Wo, bo, query_inputs, gamma,
                     accum_out=squares[it][:, c:c + 1],
                 )
 
-        def var_v(it):
+        def var_g(it):
             varsum[it] = small("varsum")
-            nc.vector.tensor_scalar(
+            nc.gpsimd.tensor_scalar(
                 out=varsum[it][:], in0=squares[it][:, 0:1], scalar1=squares[it][:, 1:2], scalar2=D * LN_EPS,
                 op0=ALU.add, op1=ALU.add,
             )
 
-        def sqrt_s(it):
-            std[it] = small("std")
-            nc.scalar.activation(out=std[it][:], in_=varsum[it][:], func=ACT.Sqrt, scale=1.0 / D)
-
-        def recip_v(it):
+        def rsqrt_s(it):
             rstd[it] = small("rstd")
-            nc.vector.reciprocal(out=rstd[it][:], in_=std[it][:])
+            nc.scalar.activation(out=rstd[it][:], in_=varsum[it][:], func=ACT.Abs_reciprocal_sqrt, scale=1.0 / D)
 
         def center(it, c):
             if c == 0:
                 centred[it] = tailp.tile([P, D], F32, name="t", tag="t")
+            if it in mean:
+                shift, op0 = mean[it][:, 0:1], ALU.subtract
+            else:
+                shift, op0 = negmean[it][:], ALU.add
             nc.vector.scalar_tensor_tensor(
-                out=centred[it][:, BANK * c:BANK * (c + 1)], in0=xT[it, c][:], scalar=negmean[it][:],
-                in1=g_bc[:, BANK * c:BANK * (c + 1)], op0=ALU.add, op1=ALU.mult,
+                out=centred[it][:, BANK * c:BANK * (c + 1)], in0=xT[it, c][:], scalar=shift,
+                in1=g_bc[:, BANK * c:BANK * (c + 1)], op0=op0, op1=ALU.mult,
             )
 
         def pieces(it):
@@ -421,35 +420,31 @@ def tile_multiheadattentionunit_pa_kernel(tc, attn, Wo, bo, query_inputs, gamma,
 
         stats_v(0)
         sum_s(1)
-        sqrt_s(0)
+        rsqrt_s(0)
         center(0, 0)
         center(0, 1)
-        mean_v(1)
+        mean_g(1)
         squares_s(1)
-        recip_v(0)
         scale_shift(0)
         cast(0)
         stats_v(2)
-        var_v(1)
-        sqrt_s(1)
-        sqrt_s(2)
+        var_g(1)
+        rsqrt_s(1)
+        rsqrt_s(2)
         center(1, 0)
         center(1, 1)
-        recip_v(1)
         sum_s(3)
         scale_shift(1)
-        mean_v(3)
+        mean_g(3)
         squares_s(3)
-        recip_v(2)
         center(2, 0)
         center(2, 1)
         cast(1)
         scale_shift(2)
-        var_v(3)
-        sqrt_s(3)
+        var_g(3)
+        rsqrt_s(3)
         cast(2)
         center(3, 0)
         center(3, 1)
-        recip_v(3)
         scale_shift(3)
         cast(3)

@@ -28,6 +28,7 @@ Y_SCALE = 220.0
 SHARES = {
     0: ((("V", 0, 512), ("S", 512, 1024)), (("V", 0, 512), ("S", 512, 1024))),
     1: ((("S", 0, 512), ("G", 512, 768), ("G", 768, 1024)), (("S", 0, 512), ("V", 512, 1024))),
+    2: ((("S", 0, 1024),), (("S", 0, 256), ("G", 256, 512), ("G", 512, 768), ("V", 768, 1024))),
 }
 SHARE = ((("S", 0, 1024),), (("S", 0, 256), ("G", 256, 640), ("G", 640, 1024)))
 CALLS = {
@@ -36,6 +37,7 @@ CALLS = {
     7: (((0, 512), (512, 1024)), ((0, 512), (512, 1024))),
 }
 CALL = (((0, 1024),), ((0, 1024),))
+N_START = 4
 N_WARM = 4
 HOLD = 3
 S_RUNS = ((6, 5, 8), (7, 0, 2))
@@ -61,10 +63,11 @@ def tile_multiheadattentionunit_pa_kernel(tc, attn, Wo, bo, query_inputs, gamma,
         x_sb, w_raw, wg, ga, tp = {}, {}, {}, {}, {}
         wc, wsc, ac, asc, mm, xT = {}, {}, {}, {}, {}, {}
 
-        def load_a(h):
-            x_sb[h] = xpool.tile([P, NIT, K], BF16, name="x_sb", tag="x_sb")
+        def load_a(h, batches=(0, 1)):
+            if h not in x_sb:
+                x_sb[h] = xpool.tile([P, NIT, K], BF16, name="x_sb", tag="x_sb")
             if h < 2:
-                for b in range(B):
+                for b in batches:
                     nc.sync.dma_start(
                         out=x_sb[h][:, 2 * b:2 * b + 2, :],
                         in_=attn[b, h, :, :].rearrange("(p i) k -> p i k", i=2),
@@ -149,6 +152,14 @@ def tile_multiheadattentionunit_pa_kernel(tc, attn, Wo, bo, query_inputs, gamma,
                 in_=ga[h][:].rearrange("p g n -> p (g n)"),
             )
 
+        def quant_a_batch(h, b):
+            for g in range(NG):
+                nc.vector.quantize_mx(
+                    out=ac[h][:, g, S * b:S * (b + 1)].bitcast(FP8X4),
+                    scales=asc[h][:, g, S * b:S * (b + 1)],
+                    in_=ga[h][:, g, PACK * S * b:PACK * S * (b + 1)],
+                )
+
         def warm_up(h):
             mm[h, 0] = mmp.tile([P, NTOK], F32, name="mm", tag="mm")
             for r in range(N_WARM):
@@ -206,20 +217,29 @@ def tile_multiheadattentionunit_pa_kernel(tc, attn, Wo, bo, query_inputs, gamma,
         posb = const.tile([P, H * NJ], F32, name="posb")
         r_sb = {}
 
-        loads(0)
+        load_a(0, (0,))
+        load_w(0, 0)
+        load_a(0, (1,))
+        load_w(0, 1)
         nc.sync.dma_start(out=bo_rows[0:H * NJ, :], in_=bo.rearrange("h (j p) -> (h j) p", p=P))
         loads(1)
         loads(2)
 
-        transposes(0)
-        copies_out(0)
+        scratch = mmp.tile([P, NTOK], F32, name="scratch", tag="mm")
+        for r in range(N_START):
+            nc.tensor.matmul(out=scratch[:], lhsT=ident_b[:], rhs=zeros[:], start=True, stop=True)
         new_wg(0, 0)
         new_wg(0, 1)
         new_codes(0)
+        transposes(0, (0,))
+        copies_out(0, (0,))
         interleave(0, 0, "V")
         interleave(0, 0, "S")
-        quant_a(0)
+        quant_a_batch(0, 0)
+        transposes(0, (1,))
+        copies_out(0, (1,))
         quant_w(0, 0)
+        quant_a_batch(0, 1)
         interleave(0, 1, "V")
         interleave(0, 1, "S")
         quant_w(0, 1)
@@ -236,8 +256,11 @@ def tile_multiheadattentionunit_pa_kernel(tc, attn, Wo, bo, query_inputs, gamma,
                 out=negbsum[:, j0:j1], in0=negbsum[:, j0:j1], in1=posb[:, NJ * h + j0:NJ * h + j1], op=ALU.add,
             )
         loads(3)
-        transposes(1)
-        copies_out(1)
+        transposes(1, (0,))
+        copies_out(1, (0,))
+        matmuls(0, 0)
+        transposes(1, (1,))
+        copies_out(1, (1,))
         new_wg(1, 0)
         interleave(1, 0, "S")
         interleave(1, 0, "G")
@@ -247,7 +270,8 @@ def tile_multiheadattentionunit_pa_kernel(tc, attn, Wo, bo, query_inputs, gamma,
 
         for s in range(H - 2):
             for j in range(NJ - HOLD):
-                matmuls(s, j)
+                if (s, j) != (0, 0):
+                    matmuls(s, j)
                 epilogue(s, j)
             for j in range(NJ - HOLD, NJ):
                 matmuls(s, j)

@@ -30,7 +30,7 @@ SHARES = {
     1: ((("S", 0, 512), ("G", 512, 768), ("G", 768, 1024)), (("S", 0, 512), ("V", 512, 1024))),
     2: ((("S", 0, 1024),), (("S", 0, 256), ("G", 256, 512), ("G", 512, 768), ("V", 768, 1024))),
 }
-SHARE = ((("S", 0, 1024),), (("S", 0, 256), ("G", 256, 640), ("G", 640, 1024)))
+SHARE = ((("S", 0, 1024),), (("S", 0, 320), ("G", 320, 672), ("G", 672, 1024)))
 CALLS = {
     0: (((0, 512), (512, 1024)), ((0, 512), (512, 1024))),
     1: (((0, 512), (512, 1024)), ((0, 512), (512, 1024))),

@@ -215,6 +215,7 @@ def tile_multiheadattentionunit_pa_kernel(tc, attn, Wo, bo, query_inputs, gamma,
         negb = const.tile([P, H * NJ], F32, name="negb")
         negbsum = const.tile([P, NJ], F32, name="negbsum")
         posb = const.tile([P, H * NJ], F32, name="posb")
+        gate = const.tile([P, NJ], F32, name="gate")
         r_sb = {}
 
         load_a(0, (0,))
@@ -263,6 +264,7 @@ def tile_multiheadattentionunit_pa_kernel(tc, attn, Wo, bo, query_inputs, gamma,
         copies_out(1, (1,))
         new_wg(1, 0)
         interleave(1, 0, "S")
+        nc.gpsimd.tensor_copy(out=gate[:], in_=negbsum[:])
         interleave(1, 0, "G")
         new_wg(1, 1)
         interleave(1, 1, "S")

@@ -165,6 +165,10 @@ def tile_multiheadattentionunit_pa_kernel(tc, attn, Wo, bo, query_inputs, gamma,
             for r in range(N_WARM):
                 nc.tensor.matmul(out=mm[h, 0][:], lhsT=ident_b[:], rhs=zeros[:], start=True, stop=True)
 
+        def wake(h, g):
+            for r in range(2):
+                nc.tensor.matmul(out=scratch[:], lhsT=ident_b[:], rhs=w_raw[h, g][:, 0, 0:BANK], start=True, stop=True)
+
         def matmuls(h, j):
             if (h, j) not in mm:
                 mm[h, j] = mmp.tile([P, NTOK], F32, name="mm", tag="mm")
@@ -237,6 +241,7 @@ def tile_multiheadattentionunit_pa_kernel(tc, attn, Wo, bo, query_inputs, gamma,
         interleave(0, 0, "V")
         interleave(0, 0, "S")
         quant_a_batch(0, 0)
+        wake(0, 0)
         transposes(0, (1,))
         copies_out(0, (1,))
         quant_w(0, 0)
@@ -244,6 +249,7 @@ def tile_multiheadattentionunit_pa_kernel(tc, attn, Wo, bo, query_inputs, gamma,
         interleave(0, 1, "V")
         interleave(0, 1, "S")
         quant_w(0, 1)
+        wake(0, 1)
         bT = mmp.tile([P, P], BF16, name="bT", tag="mm")
         nc.tensor.transpose(bT[:], bo_rows[:], ident_b[:])
         nc.vector.tensor_scalar(out=negb[:], in0=bT[:, 0:H * NJ], scalar1=-1.0, scalar2=None, op0=ALU.mult)
@@ -360,26 +366,20 @@ def tile_multiheadattentionunit_pa_kernel(tc, attn, Wo, bo, query_inputs, gamma,
             st = stat.tile([P, 2, 6], F32, name="st", tag="st")
             for c in range(2):
                 nc.vector.bn_stats(out=st[:, c, :], in_=xT[it, c][:])
-            mv = stat.tile([P, 2], F32, name="mv", tag="mv")
-            nc.vector.bn_aggr(out=mv[:], in_=st[:].rearrange("p c s -> p (c s)"))
-            mean[it] = mv
-            varsum[it] = small("varsum")
-            nc.vector.tensor_scalar(
-                out=varsum[it][:], in0=mv[:, 1:2], scalar1=float(D), scalar2=D * LN_EPS, op0=ALU.mult, op1=ALU.add,
-            )
+            mean[it] = stat.tile([P, 2], F32, name="mv", tag="mv")
+            nc.vector.bn_aggr(out=mean[it][:], in_=st[:].rearrange("p c s -> p (c s)"))
 
         def sum_s(it):
             sums[it] = stat.tile([P, 2], F32, name="sm", tag="sm")
             for c in range(2):
                 junk = tailp.tile([P, BANK], F32, name="junk", tag="junk")
-                nc.scalar.activation(out=junk[:], in_=xT[it, c][:], func=ACT.Copy, accum_out=sums[it][:, c:c + 1])
+                nc.scalar.activation(
+                    out=junk[:], in_=xT[it, c][:], func=ACT.Copy, scale=-1.0 / D, accum_out=sums[it][:, c:c + 1],
+                )
 
-        def mean_g(it):
+        def mean_s(it):
             negmean[it] = small("negmean")
-            nc.gpsimd.tensor_scalar(
-                out=negmean[it][:], in0=sums[it][:, 0:1], scalar1=sums[it][:, 1:2], scalar2=-1.0 / D,
-                op0=ALU.add, op1=ALU.mult,
-            )
+            nc.scalar.activation(out=negmean[it][:], in_=sums[it][:, 0:1], func=ACT.Identity, bias=sums[it][:, 1:2])
 
         def squares_s(it):
             squares[it] = stat.tile([P, 2], F32, name="sq", tag="sq")
@@ -390,16 +390,19 @@ def tile_multiheadattentionunit_pa_kernel(tc, attn, Wo, bo, query_inputs, gamma,
                     accum_out=squares[it][:, c:c + 1],
                 )
 
-        def var_g(it):
+        def part_s(it):
             varsum[it] = small("varsum")
-            nc.gpsimd.tensor_scalar(
-                out=varsum[it][:], in0=squares[it][:, 0:1], scalar1=squares[it][:, 1:2], scalar2=D * LN_EPS,
-                op0=ALU.add, op1=ALU.add,
-            )
+            nc.scalar.activation(out=varsum[it][:], in_=squares[it][:, 1:2], func=ACT.Copy, scale=1.0 / D, bias=LN_EPS)
 
         def rsqrt_s(it):
             rstd[it] = small("rstd")
-            nc.scalar.activation(out=rstd[it][:], in_=varsum[it][:], func=ACT.Abs_reciprocal_sqrt, scale=1.0 / D)
+            if it in mean:
+                nc.scalar.activation(out=rstd[it][:], in_=mean[it][:, 1:2], func=ACT.Abs_reciprocal_sqrt, bias=LN_EPS)
+            else:
+                nc.scalar.activation(
+                    out=rstd[it][:], in_=squares[it][:, 0:1], func=ACT.Abs_reciprocal_sqrt, scale=1.0 / D,
+                    bias=varsum[it][:],
+                )
 
         def center(it, c):
             if c == 0:
@@ -445,30 +448,30 @@ def tile_multiheadattentionunit_pa_kernel(tc, attn, Wo, bo, query_inputs, gamma,
             nc.sync.dma_start(out=rows(out_1, it), in_=codes8[it][:].bitcast(U8))
 
         stats_v(0)
-        sum_s(1)
         rsqrt_s(0)
+        sum_s(1)
         center(0, 0)
         center(0, 1)
-        mean_g(1)
+        mean_s(1)
         squares_s(1)
         scale_shift(0)
+        part_s(1)
         cast(0)
         stats_v(2)
-        var_g(1)
         rsqrt_s(1)
         rsqrt_s(2)
         center(1, 0)
         center(1, 1)
         sum_s(3)
         scale_shift(1)
-        mean_g(3)
+        mean_s(3)
         squares_s(3)
         center(2, 0)
         center(2, 1)
+        part_s(3)
+        rsqrt_s(3)
         cast(1)
         scale_shift(2)
-        var_g(3)
-        rsqrt_s(3)
         cast(2)
         center(3, 0)
         center(3, 1)

@@ -277,11 +277,12 @@ def tile_multiheadattentionunit_pa_kernel(tc, attn, Wo, bo, query_inputs, gamma,
         interleave(1, 1, "G")
 
         for s in range(H - 2):
-            for j in range(NJ - HOLD):
+            hold = 2 if s == 0 else HOLD
+            for j in range(NJ - hold):
                 if (s, j) != (0, 0):
                     matmuls(s, j)
                 epilogue(s, j)
-            for j in range(NJ - HOLD, NJ):
+            for j in range(NJ - hold, NJ):
                 matmuls(s, j)
             transposes(s + 2)
             copies_out(s + 2)
@@ -306,7 +307,7 @@ def tile_multiheadattentionunit_pa_kernel(tc, attn, Wo, bo, query_inputs, gamma,
             interleave(s + 2, 1, "G")
             interleave(s + 2, 0, "S")
             interleave(s + 2, 1, "S")
-            for j in range(NJ - HOLD, NJ):
+            for j in range(NJ - hold, NJ):
                 epilogue(s, j)
 
         def residual(it, pool, tag):

from contextlib import ExitStack

import concourse.mybir as mybir
from concourse.masks import make_identity

B, H, S, K, D = 2, 8, 256, 1024, 1024
FLOPS = 2 * B * H * S * K * D

F32 = mybir.dt.float32
BF16 = mybir.dt.bfloat16
U32 = mybir.dt.uint32
U8 = mybir.dt.uint8
FP8X4 = mybir.dt.float8_e4m3fn_x4
FP8 = mybir.dt.float8_e4m3fn
ALU = mybir.AluOpType
ACT = mybir.ActivationFunctionType

P = 128
PACK = 4
BANK = 512
NTOK = B * S
NJ = D // P
NG = K // (P * PACK)
NIT = NTOK // P
LN_EPS = 1e-3
Y_SCALE = 220.0

SHARES = {
    0: ((("V", 0, 512), ("S", 512, 1024)), (("V", 0, 512), ("S", 512, 1024))),
    1: ((("S", 0, 512), ("G", 512, 768), ("G", 768, 1024)), (("S", 0, 512), ("V", 512, 1024))),
    2: ((("S", 0, 1024),), (("S", 0, 256), ("G", 256, 512), ("G", 512, 768), ("V", 768, 1024))),
}
SHARE = ((("S", 0, 1024),), (("S", 0, 320), ("G", 320, 672), ("G", 672, 1024)))
CALLS = {
    0: (((0, 512), (512, 1024)), ((0, 512), (512, 1024))),
    1: (((0, 512), (512, 1024)), ((0, 512), (512, 1024))),
    7: (((0, 512), (512, 1024)), ((0, 512), (512, 1024))),
}
CALL = (((0, 1024),), ((0, 1024),))
N_START = 4
N_WARM = 4
HOLD = 3
S_RUNS = ((6, 5, 8), (7, 0, 2))
S_SET = frozenset((h, j) for h, j0, j1 in S_RUNS for j in range(j0, j1))


def tile_multiheadattentionunit_pa_kernel(tc, attn, Wo, bo, query_inputs, gamma, beta, out_0, out_1):
    nc = tc.nc
    with ExitStack() as ctx:
        const = ctx.enter_context(tc.tile_pool(name="const", bufs=1))
        xpool = ctx.enter_context(tc.tile_pool(name="xpool", bufs=3))
        wpool = ctx.enter_context(tc.tile_pool(name="wpool", bufs=6))
        g0pool = ctx.enter_context(tc.tile_pool(name="g0pool", bufs=2))
        g1pool = ctx.enter_context(tc.tile_pool(name="g1pool", bufs=1))
        gapool = ctx.enter_context(tc.tile_pool(name="gapool", bufs=2))
        cpool = ctx.enter_context(tc.tile_pool(name="cpool", bufs=2))
        tailp = ctx.enter_context(tc.tile_pool(name="tailp", bufs=4))
        stat = ctx.enter_context(tc.tile_pool(name="stat", bufs=4))
        tpp = ctx.enter_context(tc.psum_pool(name="tpp", bufs=4))
        mmp = ctx.enter_context(tc.psum_pool(name="mmp", bufs=4))
        ctx.enter_context(tc.manual_schedule())

        x_sb, w_raw, wg, ga, tp = {}, {}, {}, {}, {}
        wc, wsc, ac, asc, mm, xT = {}, {}, {}, {}, {}, {}

        def load_a(h, batches=(0, 1)):
            if h not in x_sb:
                x_sb[h] = xpool.tile([P, NIT, K], BF16, name="x_sb", tag="x_sb")
            if h < 2:
                for b in batches:
                    nc.sync.dma_start(
                        out=x_sb[h][:, 2 * b:2 * b + 2, :],
                        in_=attn[b, h, :, :].rearrange("(p i) k -> p i k", i=2),
                    )
            else:
                nc.sync.dma_start(
                    out=x_sb[h][:].rearrange("p (b i) k -> p b (i k)", b=B),
                    in_=attn[:, h, :, :].rearrange("b (p i) k -> p b (i k)", i=2),
                )

        def load_w(h, g):
            w_raw[h, g] = wpool.tile([P, PACK, D], BF16, name="w_raw", tag="w_raw")
            nc.sync.dma_start(
                out=w_raw[h, g][:],
                in_=Wo[h, 512 * g:512 * (g + 1), :].rearrange("(p t) d -> p t d", t=PACK),
            )

        def loads(h):
            if h < H:
                load_a(h)
                load_w(h, 0)
                load_w(h, 1)

        def transposes(h, batches=(0, 1)):
            for b in batches:
                for g in range(NG):
                    tp[h, g, b] = tpp.tile([P, 2, 2 * P], F32, name="tp", tag="tp")
                    for i in range(2):
                        words = x_sb[h][:, 2 * b + i, :].bitcast(F32)
                        for u in range(2):
                            nc.tensor.transpose(
                                tp[h, g, b][:, u, P * i:P * (i + 1)],
                                words[:, 256 * g + u:256 * (g + 1):2],
                                ident_f[:],
                            )

        def copies_out(h, batches=(0, 1)):
            if h not in ga:
                ga[h] = gapool.tile([P, NG, PACK * NTOK], BF16, name="ga", tag="ga", align_bytes=64)
            for b in batches:
                for g in range(NG):
                    nc.scalar.copy(
                        out=ga[h][:, g, :].bitcast(F32)[:, BANK * b:BANK * (b + 1)].rearrange("p (n u) -> p n u", u=2),
                        in_=tp[h, g, b][:].rearrange("p u n -> p n u"),
                    )

        def new_wg(h, g):
            pool = g0pool if g == 0 else g1pool
            wg[h, g] = pool.tile([P, D, PACK], BF16, name="wg%d" % g, tag="wg%d" % g, align_bytes=64)

        def interleave(h, g, who):
            for eng, d0, d1 in SHARES.get(h, SHARE)[g]:
                if eng != who:
                    continue
                dst = wg[h, g][:, d0:d1, :].rearrange("p (c i) t -> p c t i", i=4)
                src = w_raw[h, g][:, :, d0:d1].rearrange("p t (c i) -> p c t i", i=4)
                if eng == "S":
                    nc.scalar.copy(out=dst, in_=src)
                elif eng == "V":
                    nc.vector.tensor_copy(out=dst, in_=src)
                else:
                    nc.gpsimd.tensor_scalar(out=dst, in0=src, scalar1=1.0, scalar2=0.0, op0=ALU.mult, op1=ALU.add)

        def new_codes(h):
            wc[h] = cpool.tile([P, NG, D], U32, name="wc", tag="wc", align_bytes=64)
            wsc[h] = cpool.tile([P, NG, D], U8, name="wsc", tag="wsc", align_bytes=64)
            ac[h] = cpool.tile([P, NG, NTOK], U32, name="ac", tag="ac", align_bytes=64)
            asc[h] = cpool.tile([P, NG, NTOK], U8, name="asc", tag="asc", align_bytes=64)

        def quant_w(h, g, parts=slice(None)):
            for d0, d1 in CALLS.get(h, CALL)[g][parts]:
                nc.vector.quantize_mx(
                    out=wc[h][:, g, d0:d1].bitcast(FP8X4),
                    scales=wsc[h][:, g, d0:d1],
                    in_=wg[h, g][:, d0:d1, :].rearrange("p d t -> p (d t)"),
                )

        def quant_a(h):
            nc.vector.quantize_mx(
                out=ac[h][:].rearrange("p g n -> p (g n)").bitcast(FP8X4),
                scales=asc[h][:].rearrange("p g n -> p (g n)"),
                in_=ga[h][:].rearrange("p g n -> p (g n)"),
            )

        def quant_a_batch(h, b):
            for g in range(NG):
                nc.vector.quantize_mx(
                    out=ac[h][:, g, S * b:S * (b + 1)].bitcast(FP8X4),
                    scales=asc[h][:, g, S * b:S * (b + 1)],
                    in_=ga[h][:, g, PACK * S * b:PACK * S * (b + 1)],
                )

        def warm_up(h):
            mm[h, 0] = mmp.tile([P, NTOK], F32, name="mm", tag="mm")
            for r in range(N_WARM):
                nc.tensor.matmul(out=mm[h, 0][:], lhsT=ident_b[:], rhs=zeros[:], start=True, stop=True)

        def wake(h, g):
            for r in range(2):
                nc.tensor.matmul(out=scratch[:], lhsT=ident_b[:], rhs=w_raw[h, g][:, 0, 0:BANK], start=True, stop=True)

        def matmuls(h, j):
            if (h, j) not in mm:
                mm[h, j] = mmp.tile([P, NTOK], F32, name="mm", tag="mm")
            for g in range(NG):
                nc.tensor.matmul_mx(
                    out=mm[h, j][:],
                    lhsT=wc[h][:, g, P * j:P * (j + 1)].bitcast(FP8X4),
                    lhsT_scale=wsc[h][:, g, P * j:P * (j + 1)],
                    rhs=ac[h][:, g, :].bitcast(FP8X4),
                    rhs_scale=asc[h][:, g, :],
                    start=(g == 0),
                    stop=(g == NG - 1),
                )

        def epilogue(h, j):
            col = NJ * h + j
            if (h, j) in S_SET:
                r_sb[h, j] = const.tile([P, NTOK], F32, name="r_sb%d_%d" % (h, j))
                nc.scalar.activation(out=r_sb[h, j][:], in_=mm[h, j][:], func=ACT.Relu, bias=posb[:, col:col + 1])
            elif h == min(hh for hh in range(H) if (hh, j) not in S_SET):
                nc.vector.tensor_scalar(
                    out=acc[j][:], in0=mm[h, j][:],
                    scalar1=negb[:, col:col + 1], scalar2=negbsum[:, j:j + 1],
                    op0=ALU.max, op1=ALU.subtract,
                )
            else:
                nc.vector.scalar_tensor_tensor(
                    out=acc[j][:], in0=mm[h, j][:], scalar=negb[:, col:col + 1], in1=acc[j][:],
                    op0=ALU.max, op1=ALU.add,
                )

        ident_f = const.tile([P, P], F32, name="ident_f")
        make_identity(nc, ident_f[:])
        ident_b = const.tile([P, P], BF16, name="ident_b")
        make_identity(nc, ident_b[:])
        one = const.tile([P, 1], F32, name="one")
        nc.vector.memset(one[:], 1.0)
        warm = const.tile([P, 1], F32, name="warm")
        nc.scalar.activation(out=warm[:], in_=one[:], func=ACT.Abs_reciprocal_sqrt)
        zeros = const.tile([P, NTOK], BF16, name="zeros")
        nc.vector.memset(zeros[:], 0.0)
        bo_rows = const.tile([P, P], BF16, name="bo_rows")
        nc.vector.memset(bo_rows[:], 0.0)
        acc = [const.tile([P, NTOK], F32, name="acc%d" % j) for j in range(NJ)]
        q_sb = const.tile([P, NIT, D], BF16, name="q_sb")
        g_bc = const.tile([P, D], BF16, name="g_bc")
        b_bc = const.tile([P, D], BF16, name="b_bc")
        negb = const.tile([P, H * NJ], F32, name="negb")
        negbsum = const.tile([P, NJ], F32, name="negbsum")
        posb = const.tile([P, H * NJ], F32, name="posb")
        gate = const.tile([P, NJ], F32, name="gate")
        r_sb = {}

        load_a(0, (0,))
        load_w(0, 0)
        load_a(0, (1,))
        load_w(0, 1)
        nc.sync.dma_start(out=bo_rows[0:H * NJ, :], in_=bo.rearrange("h (j p) -> (h j) p", p=P))
        loads(1)
        loads(2)

        scratch = mmp.tile([P, NTOK], F32, name="scratch", tag="mm")
        for r in range(N_START):
            nc.tensor.matmul(out=scratch[:], lhsT=ident_b[:], rhs=zeros[:], start=True, stop=True)
        new_wg(0, 0)
        new_wg(0, 1)
        new_codes(0)
        transposes(0, (0,))
        copies_out(0, (0,))
        interleave(0, 0, "V")
        interleave(0, 0, "S")
        quant_a_batch(0, 0)
        wake(0, 0)
        transposes(0, (1,))
        copies_out(0, (1,))
        quant_w(0, 0)
        quant_a_batch(0, 1)
        interleave(0, 1, "V")
        interleave(0, 1, "S")
        quant_w(0, 1)
        wake(0, 1)
        bT = mmp.tile([P, P], BF16, name="bT", tag="mm")
        nc.tensor.transpose(bT[:], bo_rows[:], ident_b[:])
        nc.vector.tensor_scalar(out=negb[:], in0=bT[:, 0:H * NJ], scalar1=-1.0, scalar2=None, op0=ALU.mult)
        nc.vector.tensor_copy(out=posb[:], in_=bT[:, 0:H * NJ])
        nc.vector.tensor_reduce(
            out=negbsum[:], in_=negb[:].rearrange("p (h j) -> p j h", h=H),
            axis=mybir.AxisListType.X, op=ALU.add,
        )
        for h, j0, j1 in S_RUNS:
            nc.vector.tensor_tensor(
                out=negbsum[:, j0:j1], in0=negbsum[:, j0:j1], in1=posb[:, NJ * h + j0:NJ * h + j1], op=ALU.add,
            )
        loads(3)
        transposes(1, (0,))
        copies_out(1, (0,))
        matmuls(0, 0)
        transposes(1, (1,))
        copies_out(1, (1,))
        new_wg(1, 0)
        interleave(1, 0, "S")
        nc.gpsimd.tensor_copy(out=gate[:], in_=negbsum[:])
        interleave(1, 0, "G")
        new_wg(1, 1)
        interleave(1, 1, "S")
        interleave(1, 1, "G")

        for s in range(H - 2):
            hold = 2 if s == 0 else HOLD
            for j in range(NJ - hold):
                if (s, j) != (0, 0):
                    matmuls(s, j)
                epilogue(s, j)
            for j in range(NJ - hold, NJ):
                matmuls(s, j)
            transposes(s + 2)
            copies_out(s + 2)
            warm_up(s + 1)
            new_codes(s + 1)
            interleave(s + 1, 0, "V")
            interleave(s + 1, 1, "V")
            quant_a(s + 1)
            quant_w(s + 1, 0)
            quant_w(s + 1, 1)
            loads(s + 4)
            if s + 4 == H:
                nc.sync.dma_start(
                    out=q_sb[:].rearrange("p (b i) d -> p b (i d)", b=B),
                    in_=query_inputs.rearrange("b (p i) d -> p b (i d)", i=2),
                )
            if s + 3 == H:
                nc.sync.dma_start(out=g_bc[:], in_=gamma.partition_broadcast(P))
                nc.sync.dma_start(out=b_bc[:], in_=beta.partition_broadcast(P))
            new_wg(s + 2, 0)
            new_wg(s + 2, 1)
            interleave(s + 2, 1, "G")
            interleave(s + 2, 0, "S")
            interleave(s + 2, 1, "S")
            for j in range(NJ - hold, NJ):
                epilogue(s, j)

        def residual(it, pool, tag):
            for c in range(D // BANK):
                xT[it, c] = pool.tile([P, BANK], F32, name="xT", tag=tag)
                nc.tensor.matmul(
                    out=xT[it, c][:], lhsT=ident_b[:], rhs=q_sb[:, it, BANK * c:BANK * (c + 1)],
                    start=True, stop=False,
                )

        def transposed(it, j, srcs, close):
            for n, t_ in enumerate(srcs):
                nc.tensor.matmul(
                    out=xT[it, j // 4][:, P * (j % 4):P * (j % 4 + 1)],
                    lhsT=t_[:, P * it:P * (it + 1)],
                    rhs=ident_f[:],
                    is_transpose=True, start=False, stop=(close and n == len(srcs) - 1),
                )

        LAST = H - 1
        for j in range(NJ - HOLD):
            matmuls(LAST - 1, j)
            epilogue(LAST - 1, j)
        for j in range(NJ - HOLD, NJ):
            matmuls(LAST - 1, j)
        residual(0, tpp, "tp")
        residual(1, tpp, "tp")
        new_codes(LAST)
        quant_a(LAST)
        for half in range(2):
            for g in range(NG):
                quant_w(LAST, g, slice(half, half + 1))
        for j in range(NJ - HOLD, NJ):
            epilogue(LAST - 1, j)
        early = [j for j in range(NJ) if (LAST, j) in S_SET]
        for j in early:
            for it in range(2):
                transposed(it, j, [acc[j]], False)
        for j in range(NJ):
            matmuls(LAST, j)
            epilogue(LAST, j)
        for it in range(NIT):
            if it >= 2:
                residual(it, mmp, "mm")
            for j in range(NJ):
                srcs = [r_sb[h, j] for h in range(H) if (h, j) in S_SET]
                if it >= 2 or j not in early:
                    srcs.append(acc[j])
                transposed(it, j, srcs, j % 4 == 3)

        mean, negmean, varsum, rstd, centred, result, codes8, sums, squares = {}, {}, {}, {}, {}, {}, {}, {}, {}

        def small(name):
            return stat.tile([P, 1], F32, name=name, tag=name)

        def stats_v(it):
            st = stat.tile([P, 2, 6], F32, name="st", tag="st")
            for c in range(2):
                nc.vector.bn_stats(out=st[:, c, :], in_=xT[it, c][:])
            mean[it] = stat.tile([P, 2], F32, name="mv", tag="mv")
            nc.vector.bn_aggr(out=mean[it][:], in_=st[:].rearrange("p c s -> p (c s)"))

        def sum_s(it):
            sums[it] = stat.tile([P, 2], F32, name="sm", tag="sm")
            for c in range(2):
                junk = tailp.tile([P, BANK], F32, name="junk", tag="junk")
                nc.scalar.activation(
                    out=junk[:], in_=xT[it, c][:], func=ACT.Copy, scale=-1.0 / D, accum_out=sums[it][:, c:c + 1],
                )

        def mean_s(it):
            negmean[it] = small("negmean")
            nc.scalar.activation(out=negmean[it][:], in_=sums[it][:, 0:1], func=ACT.Identity, bias=sums[it][:, 1:2])

        def squares_s(it):
            squares[it] = stat.tile([P, 2], F32, name="sq", tag="sq")
            for c in range(2):
                junk = tailp.tile([P, BANK], F32, name="junk", tag="junk")
                nc.scalar.activation(
                    out=junk[:], in_=xT[it, c][:], func=ACT.Square, bias=negmean[it][:],
                    accum_out=squares[it][:, c:c + 1],
                )

        def part_s(it):
            varsum[it] = small("varsum")
            nc.scalar.activation(out=varsum[it][:], in_=squares[it][:, 1:2], func=ACT.Copy, scale=1.0 / D, bias=LN_EPS)

        def rsqrt_s(it):
            rstd[it] = small("rstd")
            if it in mean:
                nc.scalar.activation(out=rstd[it][:], in_=mean[it][:, 1:2], func=ACT.Abs_reciprocal_sqrt, bias=LN_EPS)
            else:
                nc.scalar.activation(
                    out=rstd[it][:], in_=squares[it][:, 0:1], func=ACT.Abs_reciprocal_sqrt, scale=1.0 / D,
                    bias=varsum[it][:],
                )

        def center(it, c):
            if c == 0:
                centred[it] = tailp.tile([P, D], F32, name="t", tag="t")
            if it in mean:
                shift, op0 = mean[it][:, 0:1], ALU.subtract
            else:
                shift, op0 = negmean[it][:], ALU.add
            nc.vector.scalar_tensor_tensor(
                out=centred[it][:, BANK * c:BANK * (c + 1)], in0=xT[it, c][:], scalar=shift,
                in1=g_bc[:, BANK * c:BANK * (c + 1)], op0=op0, op1=ALU.mult,
            )

        def pieces(it):
            if it < NIT - 1:
                return (slice(0, D),)
            return (slice(0, D // 2), slice(D // 2, D))

        def rows(out, it):
            return out[it // 2, :, :].rearrange("(p i) d -> p i d", i=2)[:, it % 2, :]

        def scale_shift(it):
            result[it] = tailp.tile([P, D], F32, name="o", tag="o")
            for cols in pieces(it):
                nc.vector.scalar_tensor_tensor(
                    out=result[it][:, cols], in0=centred[it][:, cols], scalar=rstd[it][:], in1=b_bc[:, cols],
                    op0=ALU.mult, op1=ALU.add,
                )
                nc.sync.dma_start(out=rows(out_0, it)[:, cols], in_=result[it][:, cols])

        def cast(it):
            codes8[it] = tailp.tile([P, D], FP8, name="o8", tag="o8")
            for n, cols in enumerate(pieces(it)):
                if n == 1:
                    nc.vector.tensor_scalar(
                        out=codes8[it][:, cols], in0=result[it][:, cols], scalar1=Y_SCALE, scalar2=None, op0=ALU.mult,
                        saturate=False,
                    )
                else:
                    nc.scalar.activation(
                        out=codes8[it][:, cols], in_=result[it][:, cols], func=ACT.Copy, scale=Y_SCALE, saturate=False,
                    )
            nc.sync.dma_start(out=rows(out_1, it), in_=codes8[it][:].bitcast(U8))

        stats_v(0)
        rsqrt_s(0)
        sum_s(1)
        center(0, 0)
        center(0, 1)
        mean_s(1)
        squares_s(1)
        scale_shift(0)
        part_s(1)
        cast(0)
        stats_v(2)
        rsqrt_s(1)
        rsqrt_s(2)
        center(1, 0)
        center(1, 1)
        sum_s(3)
        scale_shift(1)
        mean_s(3)
        squares_s(3)
        center(2, 0)
        center(2, 1)
        part_s(3)
        rsqrt_s(3)
        cast(1)
        scale_shift(2)
        cast(2)
        center(3, 0)
        center(3, 1)
        scale_shift(3)
        cast(3)
